import numpy as np
import ml_dtypes

BF16 = ml_dtypes.bfloat16


def bf(x):
    return np.asarray(x, np.float32).astype(BF16)


def f32(x):
    return np.asarray(x, np.float32)


def f64(x):
    return np.asarray(x).astype(np.float64)


def striped(idx):
    return np.tile(idx.reshape(-1, 16).T, (8, 1))


C, S, N, F = 512, 2048, 1024, 1536
R2 = 8.0
EPS = 1e-12
GAIN = np.sqrt(R2 / C)


def erf(a):
    c = np.clip(a, -6.0, 6.0)
    term = c.copy()
    tot = c.copy()
    for n in range(1, 150):
        term = term * (2.0 * c * c / (2 * n + 1))
        tot = tot + term
    r = 2.0 / np.sqrt(np.pi) * np.exp(-c * c) * tot
    return np.where(np.abs(a) > 6.0, np.sign(a), r)


def gelu(v):
    return 0.5 * v * (1.0 + erf(v / np.sqrt(2.0)))


def layer(x, gam, win, b, wout):
    r = np.maximum(np.sqrt(np.sum(x * x, axis=0, keepdims=True)), EPS)
    u = x / r * np.sqrt(C) * (gam + 1.0)
    d = np.sum(u * u, axis=0, keepdims=True) - 2.0 * (win.T @ u) + np.sum(win * win, axis=0)[:, None]
    a = gelu(b - d)
    return x + wout.T @ a


def draw_layer():
    gam = f32(GAIN * (1.0 + 0.1 * np.random.standard_normal((C, 1))) - 1.0)
    win = bf(GAIN * np.random.standard_normal((C, F)))
    b = f32(2.0 * R2 + np.random.standard_normal((F, 1)))
    wout = bf(0.02 * np.random.standard_normal((F, C)))
    return gam, win, b, wout


def setup_inputs():
    emb = f32(np.random.standard_normal((C, S)))
    pos = f32(np.random.standard_normal((C, N)))
    gam1, win1, bin1, wout1 = draw_layer()
    gam2, win2, bin2, wout2 = draw_layer()
    idx = np.random.permutation(np.tile(np.arange(S), 2))[:N]
    return {"emb": emb, "pos": pos, "gam1": gam1, "win1": win1, "bin1": bin1, "wout1": wout1, "gam2": gam2, "win2": win2, "bin2": bin2, "wout2": wout2, "offs": striped(idx)}


def reference(emb, pos, gam1, win1, bin1, wout1, gam2, win2, bin2, wout2, offs):
    idx = offs[:16].T.reshape(-1)
    x = f64(emb)[:, idx] + f64(pos)
    x = layer(x, f64(gam1), f64(win1), f64(bin1), f64(wout1))
    x = layer(x, f64(gam2), f64(win2), f64(bin2), f64(wout2))
    return x

@@ -1,0 +1,170 @@
+import concourse.mybir as mybir
+
+P = 128
+C, S, N, F = 512, 2048, 1024, 1536
+CB = C // P
+FB = F // P
+PIECE = 512
+PIECES = N // PIECE
+LAYERS = 2
+EPS = 1e-12
+
+FLOPS = LAYERS * 2 * 2 * C * F * N
+
+F32, BF16, U16 = mybir.dt.float32, mybir.dt.bfloat16, mybir.dt.uint16
+ADD, SUBTRACT = mybir.AluOpType.add, mybir.AluOpType.subtract
+MULT, MAX = mybir.AluOpType.mult, mybir.AluOpType.max
+GELU = mybir.ActivationFunctionType.Gelu
+SQUARE = mybir.ActivationFunctionType.Square
+SQRT = mybir.ActivationFunctionType.Sqrt
+
+
+def block(i):
+    return slice(i * P, (i + 1) * P)
+
+
+def tile_l2distancetransformer_b_kernel(
+    tc, emb, pos, gam1, win1, bin1, wout1, gam2, win2, bin2, wout2, offs, out
+):
+    nc = tc.nc
+    gam_in, win_in = (gam1, gam2), (win1, win2)
+    bin_in, wout_in = (bin1, bin2), (wout1, wout2)
+
+    with (
+        tc.tile_pool(name="held", bufs=1) as held,
+        tc.tile_pool(name="pair", bufs=2) as pair,
+        tc.tile_pool(name="squares", bufs=4) as squares,
+        tc.tile_pool(name="args", bufs=8) as args,
+        tc.psum_pool(name="psum_h", bufs=3) as psum_h,
+        tc.psum_pool(name="psum_acc", bufs=2) as psum_acc,
+        tc.psum_pool(name="psum_sum", bufs=1) as psum_sum,
+    ):
+        offsets = held.tile([P, N // 16], U16, name="offsets")
+        nc.sync.dma_start(offsets[:], offs)
+
+        gam_sb = [held.tile([P, CB], F32, name=f"gam{layer}") for layer in range(LAYERS)]
+        bin_sb = [held.tile([P, FB], F32, name=f"bin{layer}") for layer in range(LAYERS)]
+        with nc.allow_non_contiguous_dma(reason="one value to a partition, block by block"):
+            for layer in range(LAYERS):
+                nc.scalar.dma_start(gam_sb[layer][:], gam_in[layer].rearrange("(b p) o -> p (b o)", p=P))
+                nc.scalar.dma_start(bin_sb[layer][:], bin_in[layer].rearrange("(b p) o -> p (b o)", p=P))
+
+        table = [held.tile([P, S], F32, name=f"table{cb}") for cb in range(CB)]
+        pos_sb = [[held.tile([P, PIECE], F32, name=f"pos{piece}_{cb}") for cb in range(CB)] for piece in range(PIECES)]
+        win_sb = [held.tile([P, CB, F], BF16, name=f"win{layer}") for layer in range(LAYERS)]
+        wout_sb = [held.tile([P, FB, C], BF16, name=f"wout{layer}") for layer in range(LAYERS)]
+
+        def load_pos(piece, cb):
+            nc.sync.dma_start(pos_sb[piece][cb][:], pos[block(cb), piece * PIECE : (piece + 1) * PIECE])
+
+        def load_win(layer):
+            for cb in range(CB):
+                nc.sync.dma_start(win_sb[layer][:, cb, :], win_in[layer][block(cb), :])
+
+        def load_wout(layer):
+            nc.sync.dma_start(wout_sb[layer][:], wout_in[layer].rearrange("(b p) c -> p b c", p=P))
+
+        for cb in range(CB):
+            nc.sync.dma_start(table[cb][:], emb[block(cb), :])
+            load_pos(0, cb)
+        load_win(0)
+        for cb in range(CB):
+            load_pos(1, cb)
+        load_wout(0)
+        load_win(1)
+        load_wout(1)
+
+        ones = held.tile([P, P], BF16, name="ones")
+        nc.vector.memset(ones[:], 1.0)
+        gain = [held.tile([P, CB], F32, name=f"gain{layer}") for layer in range(LAYERS)]
+        for layer in range(LAYERS):
+            nc.vector.tensor_scalar_add(gain[layer][:], gam_sb[layer][:], 1.0)
+
+        x = [[held.tile([P, PIECE], F32, name=f"x{piece}_{cb}") for cb in range(CB)] for piece in range(PIECES)]
+        u = [None] * PIECES
+        usq = [None] * PIECES
+        a = [None] * PIECES
+        bias = [None] * LAYERS
+
+        def embed(piece):
+            piece_offsets = offsets[:, piece * (PIECE // 16) : (piece + 1) * (PIECE // 16)]
+            for cb in range(CB):
+                nc.vector.tensor_tensor(
+                    x[piece][cb][:], table[cb][:].indirect(piece_offsets), pos_sb[piece][cb][:], ADD
+                )
+
+        def hidden_bias(layer):
+            win_sq = held.tile([P, CB, F], BF16, name="win_sq")
+            for cb in range(CB):
+                nc.scalar.activation(win_sq[:, cb, :], win_sb[layer][:, cb, :], SQUARE)
+            wsq = psum_sum.tile([P, FB], F32, name="wsq")
+            for fb in range(FB):
+                for cb in range(CB):
+                    nc.tensor.matmul(
+                        wsq[:, fb : fb + 1], win_sq[:, cb, block(fb)], ones[:, 0:1], start=cb == 0, stop=cb == CB - 1
+                    )
+            bias[layer] = held.tile([P, FB], F32, name=f"bias{layer}")
+            nc.vector.tensor_tensor(bias[layer][:], bin_sb[layer][:], wsq[:], SUBTRACT)
+
+        def normalise(layer, piece):
+            xsq_sum = psum_sum.tile([P, PIECE], F32, name="xsq_sum")
+            gsq_sum = psum_sum.tile([P, PIECE], F32, name="gsq_sum")
+            for cb in range(CB):
+                xsq = squares.tile([P, PIECE], BF16, name="xsq")
+                nc.scalar.activation(xsq[:], x[piece][cb][:], SQUARE)
+                nc.tensor.matmul(xsq_sum[:], ones[:], xsq[:], start=cb == 0, stop=cb == CB - 1)
+                gsq = squares.tile([P, PIECE], BF16, name="gsq")
+                nc.scalar.activation(gsq[:], x[piece][cb][:], SQUARE, scale=gain[layer][:, cb : cb + 1])
+                nc.tensor.matmul(gsq_sum[:], ones[:], gsq[:], start=cb == 0, stop=cb == CB - 1)
+            mean_sq = pair.tile([P, PIECE], F32, name="mean_sq")
+            nc.vector.tensor_scalar(mean_sq[:], xsq_sum[:], 1.0 / C, EPS * EPS / C, MULT, MAX)
+            inv_sq = pair.tile([P, PIECE], F32, name="inv_sq")
+            nc.vector.reciprocal(inv_sq[:], mean_sq[:])
+            inv_r = pair.tile([P, PIECE], F32, name="inv_r")
+            nc.scalar.activation(inv_r[:], inv_sq[:], SQRT)
+            usq[piece] = pair.tile([P, PIECE], F32, name="usq")
+            nc.vector.tensor_tensor(usq[piece][:], gsq_sum[:], inv_sq[:], MULT)
+            u[piece] = pair.tile([P, CB, PIECE], BF16, name="u")
+            for cb in range(CB):
+                nc.vector.scalar_tensor_tensor(
+                    u[piece][:, cb, :], x[piece][cb][:], gain[layer][:, cb : cb + 1], inv_r[:], MULT, MULT
+                )
+
+        def project_in(layer, piece):
+            a[piece] = pair.tile([P, FB, PIECE], BF16, name="a")
+            for fb in range(FB):
+                h = psum_h.tile([P, PIECE], F32, name="h")
+                for cb in range(CB):
+                    nc.tensor.matmul(
+                        h[:], win_sb[layer][:, cb, block(fb)], u[piece][:, cb, :], start=cb == 0, stop=cb == CB - 1
+                    )
+                arg = args.tile([P, PIECE], F32, name="arg")
+                nc.vector.scalar_tensor_tensor(arg[:], h[:], 2.0, usq[piece][:], MULT, SUBTRACT)
+                nc.scalar.activation(a[piece][:, fb, :], arg[:], GELU, bias=bias[layer][:, fb : fb + 1])
+
+        def project_out(layer, piece):
+            for cb in range(CB):
+                acc = psum_acc.tile([P, PIECE], F32, name="acc")
+                for fb in range(FB):
+                    nc.tensor.matmul(
+                        acc[:], wout_sb[layer][:, fb, block(cb)], a[piece][:, fb, :], start=fb == 0, stop=fb == FB - 1
+                    )
+                nc.vector.tensor_tensor(x[piece][cb][:], acc[:], x[piece][cb][:], ADD)
+
+        def store(piece):
+            for cb in range(CB):
+                nc.sync.dma_start(out[block(cb), piece * PIECE : (piece + 1) * PIECE], x[piece][cb][:])
+
+        for piece in range(PIECES):
+            embed(piece)
+            normalise(0, piece)
+        for layer in range(LAYERS):
+            hidden_bias(layer)
+            for piece in range(PIECES):
+                project_in(layer, piece)
+            for piece in range(PIECES):
+                project_out(layer, piece)
+                if layer + 1 < LAYERS:
+                    normalise(layer + 1, piece)
+                else:
+                    store(piece)

@@ -12,11 +12,10 @@ EPS = 1e-12
 FLOPS = LAYERS * 2 * 2 * C * F * N
 
 F32, BF16, U16 = mybir.dt.float32, mybir.dt.bfloat16, mybir.dt.uint16
-ADD, SUBTRACT = mybir.AluOpType.add, mybir.AluOpType.subtract
-MULT, MAX = mybir.AluOpType.mult, mybir.AluOpType.max
+ADD, SUBTRACT, MULT = mybir.AluOpType.add, mybir.AluOpType.subtract, mybir.AluOpType.mult
 GELU = mybir.ActivationFunctionType.Gelu
 SQUARE = mybir.ActivationFunctionType.Square
-SQRT = mybir.ActivationFunctionType.Sqrt
+RSQRT = mybir.ActivationFunctionType.Abs_reciprocal_sqrt
 
 
 def block(i):
@@ -32,8 +31,9 @@ def tile_l2distancetransformer_b_kernel(
 
     with (
         tc.tile_pool(name="held", bufs=1) as held,
-        tc.tile_pool(name="pair", bufs=2) as pair,
-        tc.tile_pool(name="squares", bufs=4) as squares,
+        tc.tile_pool(name="unit", bufs=1) as unit,
+        tc.tile_pool(name="squares", bufs=CB) as squares,
+        tc.tile_pool(name="win_squares", bufs=FB) as win_squares,
         tc.tile_pool(name="args", bufs=8) as args,
         tc.psum_pool(name="psum_h", bufs=3) as psum_h,
         tc.psum_pool(name="psum_acc", bufs=2) as psum_acc,
@@ -44,10 +44,11 @@ def tile_l2distancetransformer_b_kernel(
 
         gam_sb = [held.tile([P, CB], F32, name=f"gam{layer}") for layer in range(LAYERS)]
         bin_sb = [held.tile([P, FB], F32, name=f"bin{layer}") for layer in range(LAYERS)]
-        with nc.allow_non_contiguous_dma(reason="one value to a partition, block by block"):
-            for layer in range(LAYERS):
-                nc.scalar.dma_start(gam_sb[layer][:], gam_in[layer].rearrange("(b p) o -> p (b o)", p=P))
-                nc.scalar.dma_start(bin_sb[layer][:], bin_in[layer].rearrange("(b p) o -> p (b o)", p=P))
+
+        def load_vectors(layer):
+            with nc.allow_non_contiguous_dma(reason="one value to a partition, block by block"):
+                nc.sync.dma_start(gam_sb[layer][:], gam_in[layer].rearrange("(b p) o -> p (b o)", p=P))
+                nc.sync.dma_start(bin_sb[layer][:], bin_in[layer].rearrange("(b p) o -> p (b o)", p=P))
 
         table = [held.tile([P, S], F32, name=f"table{cb}") for cb in range(CB)]
         pos_sb = [[held.tile([P, PIECE], F32, name=f"pos{piece}_{cb}") for cb in range(CB)] for piece in range(PIECES)]
@@ -64,6 +65,7 @@ def tile_l2distancetransformer_b_kernel(
         def load_wout(layer):
             nc.sync.dma_start(wout_sb[layer][:], wout_in[layer].rearrange("(b p) c -> p b c", p=P))
 
+        load_vectors(0)
         for cb in range(CB):
             nc.sync.dma_start(table[cb][:], emb[block(cb), :])
             load_pos(0, cb)
@@ -71,78 +73,99 @@ def tile_l2distancetransformer_b_kernel(
         for cb in range(CB):
             load_pos(1, cb)
         load_wout(0)
+        load_vectors(1)
         load_win(1)
         load_wout(1)
 
         ones = held.tile([P, P], BF16, name="ones")
         nc.vector.memset(ones[:], 1.0)
+        warm = held.tile([P, 1], F32, name="warm")
+        nc.scalar.activation(warm[:], ones[:, 0:1], RSQRT)
         gain = [held.tile([P, CB], F32, name=f"gain{layer}") for layer in range(LAYERS)]
         for layer in range(LAYERS):
             nc.vector.tensor_scalar_add(gain[layer][:], gam_sb[layer][:], 1.0)
+        bias = [held.tile([P, FB], F32, name=f"bias{layer}") for layer in range(LAYERS)]
 
         x = [[held.tile([P, PIECE], F32, name=f"x{piece}_{cb}") for cb in range(CB)] for piece in range(PIECES)]
+        xsq = [None] * CB
+        gsq = [None] * CB
+        folded = {}
+        win_sq = [None] * FB
         u = [None] * PIECES
         usq = [None] * PIECES
         a = [None] * PIECES
-        bias = [None] * LAYERS
 
-        def embed(piece):
-            piece_offsets = offsets[:, piece * (PIECE // 16) : (piece + 1) * (PIECE // 16)]
-            for cb in range(CB):
+        def square_win(layer):
+            for fb in range(FB):
+                win_sq[fb] = win_squares.tile([P, CB, P], BF16, name="win_sq")
+                nc.gpsimd.tensor_tensor(win_sq[fb][:], win_sb[layer][:, :, block(fb)], win_sb[layer][:, :, block(fb)], MULT)
+
+        def square_block(layer, piece, cb):
+            if layer == 0:
+                piece_offsets = offsets[:, piece * (PIECE // 16) : (piece + 1) * (PIECE // 16)]
                 nc.vector.tensor_tensor(
                     x[piece][cb][:], table[cb][:].indirect(piece_offsets), pos_sb[piece][cb][:], ADD
                 )
+            xsq[cb] = squares.tile([P, PIECE], F32, name="xsq")
+            nc.scalar.activation(xsq[cb][:], x[piece][cb][:], SQUARE)
+            gsq[cb] = squares.tile([P, PIECE], F32, name="gsq")
+            nc.scalar.activation(gsq[cb][:], x[piece][cb][:], SQUARE, scale=gain[layer][:, cb : cb + 1])
 
-        def hidden_bias(layer):
-            win_sq = held.tile([P, CB, F], BF16, name="win_sq")
-            for cb in range(CB):
-                nc.scalar.activation(win_sq[:, cb, :], win_sb[layer][:, cb, :], SQUARE)
-            wsq = psum_sum.tile([P, FB], F32, name="wsq")
-            for fb in range(FB):
-                for cb in range(CB):
-                    nc.tensor.matmul(
-                        wsq[:, fb : fb + 1], win_sq[:, cb, block(fb)], ones[:, 0:1], start=cb == 0, stop=cb == CB - 1
-                    )
-            bias[layer] = held.tile([P, FB], F32, name=f"bias{layer}")
-            nc.vector.tensor_tensor(bias[layer][:], bin_sb[layer][:], wsq[:], SUBTRACT)
+        def fold_block(cb):
+            for name, terms in (("xsq", xsq), ("gsq", gsq)):
+                if 0 < cb < CB - 1:
+                    nc.vector.tensor_tensor(terms[0][:], terms[0][:], terms[cb][:], ADD)
+                if cb == CB - 1:
+                    folded[name] = unit.tile([P, PIECE], BF16, name=name + "_folded")
+                    nc.vector.tensor_tensor(folded[name][:], terms[0][:], terms[cb][:], ADD)
 
-        def normalise(layer, piece):
+        def finish_norm(layer, piece):
             xsq_sum = psum_sum.tile([P, PIECE], F32, name="xsq_sum")
+            nc.tensor.matmul(xsq_sum[:], ones[:], folded["xsq"][:], start=True, stop=True)
             gsq_sum = psum_sum.tile([P, PIECE], F32, name="gsq_sum")
-            for cb in range(CB):
-                xsq = squares.tile([P, PIECE], BF16, name="xsq")
-                nc.scalar.activation(xsq[:], x[piece][cb][:], SQUARE)
-                nc.tensor.matmul(xsq_sum[:], ones[:], xsq[:], start=cb == 0, stop=cb == CB - 1)
-                gsq = squares.tile([P, PIECE], BF16, name="gsq")
-                nc.scalar.activation(gsq[:], x[piece][cb][:], SQUARE, scale=gain[layer][:, cb : cb + 1])
-                nc.tensor.matmul(gsq_sum[:], ones[:], gsq[:], start=cb == 0, stop=cb == CB - 1)
-            mean_sq = pair.tile([P, PIECE], F32, name="mean_sq")
-            nc.vector.tensor_scalar(mean_sq[:], xsq_sum[:], 1.0 / C, EPS * EPS / C, MULT, MAX)
-            inv_sq = pair.tile([P, PIECE], F32, name="inv_sq")
-            nc.vector.reciprocal(inv_sq[:], mean_sq[:])
-            inv_r = pair.tile([P, PIECE], F32, name="inv_r")
-            nc.scalar.activation(inv_r[:], inv_sq[:], SQRT)
-            usq[piece] = pair.tile([P, PIECE], F32, name="usq")
-            nc.vector.tensor_tensor(usq[piece][:], gsq_sum[:], inv_sq[:], MULT)
-            u[piece] = pair.tile([P, CB, PIECE], BF16, name="u")
+            nc.tensor.matmul(gsq_sum[:], ones[:], folded["gsq"][:], start=True, stop=True)
+            raw_inv_r = unit.tile([P, PIECE], F32, name="raw_inv_r")
+            nc.scalar.activation(raw_inv_r[:], xsq_sum[:], RSQRT, scale=1.0 / C)
+            inv_r = unit.tile([P, PIECE], F32, name="inv_r")
+            nc.vector.tensor_scalar_min(inv_r[:], raw_inv_r[:], C**0.5 / EPS)
+            u[piece] = unit.tile([P, CB, PIECE], BF16, name="u")
             for cb in range(CB):
                 nc.vector.scalar_tensor_tensor(
                     u[piece][:, cb, :], x[piece][cb][:], gain[layer][:, cb : cb + 1], inv_r[:], MULT, MULT
                 )
+            inv_sq = unit.tile([P, PIECE], F32, name="inv_sq")
+            nc.scalar.activation(inv_sq[:], inv_r[:], SQUARE)
+            usq[piece] = unit.tile([P, PIECE], F32, name="usq")
+            nc.vector.tensor_tensor(usq[piece][:], gsq_sum[:], inv_sq[:], MULT)
 
-        def project_in(layer, piece):
-            a[piece] = pair.tile([P, FB, PIECE], BF16, name="a")
+        def project_in(layer, piece, following):
+            a[piece] = unit.tile([P, FB, PIECE], BF16, name="a")
+            if piece == 0:
+                wsq = psum_sum.tile([P, FB], F32, name="wsq")
             for fb in range(FB):
                 h = psum_h.tile([P, PIECE], F32, name="h")
                 for cb in range(CB):
                     nc.tensor.matmul(
                         h[:], win_sb[layer][:, cb, block(fb)], u[piece][:, cb, :], start=cb == 0, stop=cb == CB - 1
                     )
+                if piece == 0:
+                    for cb in range(CB):
+                        nc.tensor.matmul(
+                            wsq[:, fb : fb + 1], win_sq[fb][:, cb, :], ones[:, 0:1], start=cb == 0, stop=cb == CB - 1
+                        )
+                    nc.vector.tensor_tensor(
+                        bias[layer][:, fb : fb + 1], bin_sb[layer][:, fb : fb + 1], wsq[:, fb : fb + 1], SUBTRACT
+                    )
                 arg = args.tile([P, PIECE], F32, name="arg")
                 nc.vector.scalar_tensor_tensor(arg[:], h[:], 2.0, usq[piece][:], MULT, SUBTRACT)
                 nc.scalar.activation(a[piece][:, fb, :], arg[:], GELU, bias=bias[layer][:, fb : fb + 1])
+                if following is not None and fb % (FB // CB) == 0:
+                    square_block(following[0], following[1], fb // (FB // CB))
 
-        def project_out(layer, piece):
+        def project_out(layer, piece, following):
+            if following is not None:
+                for cb in range(CB):
+                    fold_block(cb)
             for cb in range(CB):
                 acc = psum_acc.tile([P, PIECE], F32, name="acc")
                 for fb in range(FB):
@@ -150,21 +173,20 @@ def tile_l2distancetransformer_b_kernel(
                         acc[:], wout_sb[layer][:, fb, block(cb)], a[piece][:, fb, :], start=fb == 0, stop=fb == FB - 1
                     )
                 nc.vector.tensor_tensor(x[piece][cb][:], acc[:], x[piece][cb][:], ADD)
+                if layer == LAYERS - 1:
+                    nc.sync.dma_start(out[block(cb), piece * PIECE : (piece + 1) * PIECE], x[piece][cb][:])
+                if cb == 1 and following is not None:
+                    finish_norm(following[0], following[1])
 
-        def store(piece):
-            for cb in range(CB):
-                nc.sync.dma_start(out[block(cb), piece * PIECE : (piece + 1) * PIECE], x[piece][cb][:])
-
-        for piece in range(PIECES):
-            embed(piece)
-            normalise(0, piece)
-        for layer in range(LAYERS):
-            hidden_bias(layer)
-            for piece in range(PIECES):
-                project_in(layer, piece)
-            for piece in range(PIECES):
-                project_out(layer, piece)
-                if layer + 1 < LAYERS:
-                    normalise(layer + 1, piece)
-                else:
-                    store(piece)
+        units = [(layer, piece) for layer in range(LAYERS) for piece in range(PIECES)]
+        square_win(0)
+        for cb in range(CB):
+            square_block(0, 0, cb)
+            fold_block(cb)
+        finish_norm(0, 0)
+        for k, (layer, piece) in enumerate(units):
+            following = units[k + 1] if k + 1 < len(units) else None
+            project_in(layer, piece, following)
+            if piece == 0 and layer + 1 < LAYERS:
+                square_win(layer + 1)
+            project_out(layer, piece, following)

@@ -44,11 +44,10 @@ def tile_l2distancetransformer_b_kernel(
 
         gam_sb = [held.tile([P, CB], F32, name=f"gam{layer}") for layer in range(LAYERS)]
         bin_sb = [held.tile([P, FB], F32, name=f"bin{layer}") for layer in range(LAYERS)]
-
-        def load_vectors(layer):
-            with nc.allow_non_contiguous_dma(reason="one value to a partition, block by block"):
-                nc.sync.dma_start(gam_sb[layer][:], gam_in[layer].rearrange("(b p) o -> p (b o)", p=P))
-                nc.sync.dma_start(bin_sb[layer][:], bin_in[layer].rearrange("(b p) o -> p (b o)", p=P))
+        with nc.allow_non_contiguous_dma(reason="one value to a partition, block by block"):
+            for layer in range(LAYERS):
+                nc.scalar.dma_start(gam_sb[layer][:], gam_in[layer].rearrange("(b p) o -> p (b o)", p=P))
+                nc.scalar.dma_start(bin_sb[layer][:], bin_in[layer].rearrange("(b p) o -> p (b o)", p=P))
 
         table = [held.tile([P, S], F32, name=f"table{cb}") for cb in range(CB)]
         pos_sb = [[held.tile([P, PIECE], F32, name=f"pos{piece}_{cb}") for cb in range(CB)] for piece in range(PIECES)]
@@ -65,7 +64,6 @@ def tile_l2distancetransformer_b_kernel(
         def load_wout(layer):
             nc.sync.dma_start(wout_sb[layer][:], wout_in[layer].rearrange("(b p) c -> p b c", p=P))
 
-        load_vectors(0)
         for cb in range(CB):
             nc.sync.dma_start(table[cb][:], emb[block(cb), :])
             load_pos(0, cb)
@@ -73,7 +71,6 @@ def tile_l2distancetransformer_b_kernel(
         for cb in range(CB):
             load_pos(1, cb)
         load_wout(0)
-        load_vectors(1)
         load_win(1)
         load_wout(1)
 
@@ -98,20 +95,17 @@ def tile_l2distancetransformer_b_kernel(
         def square_win(layer):
             for fb in range(FB):
                 win_sq[fb] = win_squares.tile([P, CB, P], BF16, name="win_sq")
-                nc.gpsimd.tensor_tensor(win_sq[fb][:], win_sb[layer][:, :, block(fb)], win_sb[layer][:, :, block(fb)], MULT)
+                nc.scalar.activation(win_sq[fb][:], win_sb[layer][:, :, block(fb)], SQUARE)
+
+        def embed_block(piece, cb):
+            piece_offsets = offsets[:, piece * (PIECE // 16) : (piece + 1) * (PIECE // 16)]
+            nc.vector.tensor_tensor(x[piece][cb][:], table[cb][:].indirect(piece_offsets), pos_sb[piece][cb][:], ADD)
 
         def square_block(layer, piece, cb):
-            if layer == 0:
-                piece_offsets = offsets[:, piece * (PIECE // 16) : (piece + 1) * (PIECE // 16)]
-                nc.vector.tensor_tensor(
-                    x[piece][cb][:], table[cb][:].indirect(piece_offsets), pos_sb[piece][cb][:], ADD
-                )
             xsq[cb] = squares.tile([P, PIECE], F32, name="xsq")
             nc.scalar.activation(xsq[cb][:], x[piece][cb][:], SQUARE)
             gsq[cb] = squares.tile([P, PIECE], F32, name="gsq")
             nc.scalar.activation(gsq[cb][:], x[piece][cb][:], SQUARE, scale=gain[layer][:, cb : cb + 1])
-
-        def fold_block(cb):
             for name, terms in (("xsq", xsq), ("gsq", gsq)):
                 if 0 < cb < CB - 1:
                     nc.vector.tensor_tensor(terms[0][:], terms[0][:], terms[cb][:], ADD)
@@ -138,7 +132,7 @@ def tile_l2distancetransformer_b_kernel(
             usq[piece] = unit.tile([P, PIECE], F32, name="usq")
             nc.vector.tensor_tensor(usq[piece][:], gsq_sum[:], inv_sq[:], MULT)
 
-        def project_in(layer, piece, following):
+        def project_in(layer, piece):
             a[piece] = unit.tile([P, FB, PIECE], BF16, name="a")
             if piece == 0:
                 wsq = psum_sum.tile([P, FB], F32, name="wsq")
@@ -159,13 +153,13 @@ def tile_l2distancetransformer_b_kernel(
                 arg = args.tile([P, PIECE], F32, name="arg")
                 nc.vector.scalar_tensor_tensor(arg[:], h[:], 2.0, usq[piece][:], MULT, SUBTRACT)
                 nc.scalar.activation(a[piece][:, fb, :], arg[:], GELU, bias=bias[layer][:, fb : fb + 1])
-                if following is not None and fb % (FB // CB) == 0:
-                    square_block(following[0], following[1], fb // (FB // CB))
+                if layer == 0 and piece + 1 < PIECES and fb % (FB // CB) == 0:
+                    embed_block(piece + 1, fb // (FB // CB))
 
         def project_out(layer, piece, following):
             if following is not None:
                 for cb in range(CB):
-                    fold_block(cb)
+                    square_block(following[0], following[1], cb)
             for cb in range(CB):
                 acc = psum_acc.tile([P, PIECE], F32, name="acc")
                 for fb in range(FB):
@@ -179,14 +173,14 @@ def tile_l2distancetransformer_b_kernel(
                     finish_norm(following[0], following[1])
 
         units = [(layer, piece) for layer in range(LAYERS) for piece in range(PIECES)]
-        square_win(0)
         for cb in range(CB):
+            embed_block(0, cb)
             square_block(0, 0, cb)
-            fold_block(cb)
         finish_norm(0, 0)
+        square_win(0)
         for k, (layer, piece) in enumerate(units):
             following = units[k + 1] if k + 1 < len(units) else None
-            project_in(layer, piece, following)
+            project_in(layer, piece)
+            project_out(layer, piece, following)
             if piece == 0 and layer + 1 < LAYERS:
                 square_win(layer + 1)
-            project_out(layer, piece, following)

@@ -1,4 +1,5 @@
 import concourse.mybir as mybir
+from concourse.masks import make_identity
 
 P = 128
 C, S, N, F = 512, 2048, 1024, 1536
@@ -8,6 +9,7 @@ PIECE = 512
 PIECES = N // PIECE
 LAYERS = 2
 EPS = 1e-12
+VECTOR_ROWS = LAYERS * (CB + FB)
 
 FLOPS = LAYERS * 2 * 2 * C * F * N
 
@@ -42,12 +44,21 @@ def tile_l2distancetransformer_b_kernel(
         offsets = held.tile([P, N // 16], U16, name="offsets")
         nc.sync.dma_start(offsets[:], offs)
 
-        gam_sb = [held.tile([P, CB], F32, name=f"gam{layer}") for layer in range(LAYERS)]
-        bin_sb = [held.tile([P, FB], F32, name=f"bin{layer}") for layer in range(LAYERS)]
-        with nc.allow_non_contiguous_dma(reason="one value to a partition, block by block"):
-            for layer in range(LAYERS):
-                nc.scalar.dma_start(gam_sb[layer][:], gam_in[layer].rearrange("(b p) o -> p (b o)", p=P))
-                nc.scalar.dma_start(bin_sb[layer][:], bin_in[layer].rearrange("(b p) o -> p (b o)", p=P))
+        vector_rows = held.tile([2 * VECTOR_ROWS, P], F32, name="vector_rows")
+        nc.vector.memset(vector_rows[VECTOR_ROWS:, :], 0.0)
+        for layer in range(LAYERS):
+            gam_row = layer * (CB + FB)
+            bin_row = gam_row + CB
+            nc.scalar.dma_start(vector_rows[gam_row : gam_row + CB, :], gam_in[layer].rearrange("(b p) o -> b (p o)", p=P))
+            nc.scalar.dma_start(vector_rows[bin_row : bin_row + FB, :], bin_in[layer].rearrange("(b p) o -> b (p o)", p=P))
+        identity = held.tile([2 * VECTOR_ROWS, 2 * VECTOR_ROWS], F32, name="identity")
+        make_identity(nc, identity[:])
+        flipped = psum_sum.tile([P, 2 * VECTOR_ROWS], F32, name="flipped", tag="wsq")
+        nc.tensor.transpose(flipped[:], vector_rows[:], identity[:])
+        vectors = held.tile([P, 2 * VECTOR_ROWS], F32, name="vectors")
+        nc.vector.tensor_copy(vectors[:], flipped[:])
+        gam_sb = [vectors[:, layer * (CB + FB) : layer * (CB + FB) + CB] for layer in range(LAYERS)]
+        bin_sb = [vectors[:, layer * (CB + FB) + CB : (layer + 1) * (CB + FB)] for layer in range(LAYERS)]
 
         table = [held.tile([P, S], F32, name=f"table{cb}") for cb in range(CB)]
         pos_sb = [[held.tile([P, PIECE], F32, name=f"pos{piece}_{cb}") for cb in range(CB)] for piece in range(PIECES)]

@@ -7,16 +7,20 @@ CB = C // P
 FB = F // P
 PIECE = 512
 PIECES = N // PIECE
+HALF = PIECE // 2
+HALVES = (slice(0, HALF), slice(HALF, PIECE))
 LAYERS = 2
 EPS = 1e-12
+INV_R_CAP = C**0.5 / EPS
 VECTOR_ROWS = LAYERS * (CB + FB)
 
 FLOPS = LAYERS * 2 * 2 * C * F * N
 
 F32, BF16, U16 = mybir.dt.float32, mybir.dt.bfloat16, mybir.dt.uint16
-ADD, SUBTRACT, MULT = mybir.AluOpType.add, mybir.AluOpType.subtract, mybir.AluOpType.mult
+ADD, SUBTRACT, MULT, MIN = mybir.AluOpType.add, mybir.AluOpType.subtract, mybir.AluOpType.mult, mybir.AluOpType.min
 GELU = mybir.ActivationFunctionType.Gelu
 SQUARE = mybir.ActivationFunctionType.Square
+COPY = mybir.ActivationFunctionType.Copy
 RSQRT = mybir.ActivationFunctionType.Abs_reciprocal_sqrt
 
 
@@ -39,7 +43,8 @@ def tile_l2distancetransformer_b_kernel(
         tc.tile_pool(name="args", bufs=8) as args,
         tc.psum_pool(name="psum_h", bufs=3) as psum_h,
         tc.psum_pool(name="psum_acc", bufs=2) as psum_acc,
-        tc.psum_pool(name="psum_sum", bufs=1) as psum_sum,
+        tc.psum_pool(name="psum_sum", bufs=2) as psum_sum,
+        tc.psum_pool(name="psum_wsq", bufs=1) as psum_wsq,
     ):
         offsets = held.tile([P, N // 16], U16, name="offsets")
         nc.sync.dma_start(offsets[:], offs)
@@ -53,7 +58,7 @@ def tile_l2distancetransformer_b_kernel(
             nc.scalar.dma_start(vector_rows[bin_row : bin_row + FB, :], bin_in[layer].rearrange("(b p) o -> b (p o)", p=P))
         identity = held.tile([2 * VECTOR_ROWS, 2 * VECTOR_ROWS], F32, name="identity")
         make_identity(nc, identity[:])
-        flipped = psum_sum.tile([P, 2 * VECTOR_ROWS], F32, name="flipped", tag="wsq")
+        flipped = psum_wsq.tile([P, 2 * VECTOR_ROWS], F32, name="flipped", tag="wsq")
         nc.tensor.transpose(flipped[:], vector_rows[:], identity[:])
         vectors = held.tile([P, 2 * VECTOR_ROWS], F32, name="vectors")
         nc.vector.tensor_copy(vectors[:], flipped[:])
@@ -90,13 +95,16 @@ def tile_l2distancetransformer_b_kernel(
         warm = held.tile([P, 1], F32, name="warm")
         nc.scalar.activation(warm[:], ones[:, 0:1], RSQRT)
         gain = [held.tile([P, CB], F32, name=f"gain{layer}") for layer in range(LAYERS)]
+        gain_sq = [held.tile([P, CB], F32, name=f"gain_sq{layer}") for layer in range(LAYERS)]
         for layer in range(LAYERS):
             nc.vector.tensor_scalar_add(gain[layer][:], gam_sb[layer][:], 1.0)
+            nc.vector.tensor_tensor(gain_sq[layer][:], gain[layer][:], gain[layer][:], MULT)
         bias = [held.tile([P, FB], F32, name=f"bias{layer}") for layer in range(LAYERS)]
 
         x = [[held.tile([P, PIECE], F32, name=f"x{piece}_{cb}") for cb in range(CB)] for piece in range(PIECES)]
         xsq = [None] * CB
-        gsq = [None] * CB
+        gx = [None] * CB
+        gsq_run = [None]
         folded = {}
         win_sq = [None] * FB
         u = [None] * PIECES
@@ -109,44 +117,60 @@ def tile_l2distancetransformer_b_kernel(
                 nc.scalar.activation(win_sq[fb][:], win_sb[layer][:, :, block(fb)], SQUARE)
 
         def embed_block(piece, cb):
-            piece_offsets = offsets[:, piece * (PIECE // 16) : (piece + 1) * (PIECE // 16)]
-            nc.vector.tensor_tensor(x[piece][cb][:], table[cb][:].indirect(piece_offsets), pos_sb[piece][cb][:], ADD)
+            for half in HALVES:
+                first = (piece * PIECE + half.start) // 16
+                half_offsets = offsets[:, first : first + HALF // 16]
+                nc.vector.tensor_tensor(
+                    x[piece][cb][:, half], table[cb][:].indirect(half_offsets), pos_sb[piece][cb][:, half], ADD
+                )
 
         def square_block(layer, piece, cb):
             xsq[cb] = squares.tile([P, PIECE], F32, name="xsq")
-            nc.scalar.activation(xsq[cb][:], x[piece][cb][:], SQUARE)
-            gsq[cb] = squares.tile([P, PIECE], F32, name="gsq")
-            nc.scalar.activation(gsq[cb][:], x[piece][cb][:], SQUARE, scale=gain[layer][:, cb : cb + 1])
-            for name, terms in (("xsq", xsq), ("gsq", gsq)):
-                if 0 < cb < CB - 1:
-                    nc.vector.tensor_tensor(terms[0][:], terms[0][:], terms[cb][:], ADD)
-                if cb == CB - 1:
-                    folded[name] = unit.tile([P, PIECE], BF16, name=name + "_folded")
-                    nc.vector.tensor_tensor(folded[name][:], terms[0][:], terms[cb][:], ADD)
+            block_gain_sq = gain_sq[layer][:, cb : cb + 1]
+            if cb == 0:
+                gsq_run[0] = unit.tile([P, PIECE], F32, name="gsq_run")
+            if cb == CB - 1:
+                folded["xsq"] = unit.tile([P, PIECE], BF16, name="xsq_folded")
+                folded["gsq"] = unit.tile([P, PIECE], BF16, name="gsq_folded")
+            for half in HALVES:
+                nc.scalar.activation(xsq[cb][:, half], x[piece][cb][:, half], SQUARE)
+                if cb == 0:
+                    nc.vector.tensor_scalar_mul(gsq_run[0][:, half], xsq[0][:, half], block_gain_sq)
+                elif cb < CB - 1:
+                    nc.vector.scalar_tensor_tensor(
+                        gsq_run[0][:, half], xsq[cb][:, half], block_gain_sq, gsq_run[0][:, half], MULT, ADD
+                    )
+                    nc.vector.tensor_tensor(xsq[0][:, half], xsq[0][:, half], xsq[cb][:, half], ADD)
+                else:
+                    nc.vector.tensor_tensor(folded["xsq"][:, half], xsq[0][:, half], xsq[cb][:, half], ADD)
+            if cb == CB - 1:
+                nc.vector.scalar_tensor_tensor(folded["gsq"][:], xsq[cb][:], block_gain_sq, gsq_run[0][:], MULT, ADD)
+            gx[cb] = squares.tile([P, PIECE], F32, name="gx")
+            nc.scalar.activation(gx[cb][:], x[piece][cb][:], COPY, scale=gain[layer][:, cb : cb + 1])
 
         def finish_norm(layer, piece):
-            xsq_sum = psum_sum.tile([P, PIECE], F32, name="xsq_sum")
-            nc.tensor.matmul(xsq_sum[:], ones[:], folded["xsq"][:], start=True, stop=True)
-            gsq_sum = psum_sum.tile([P, PIECE], F32, name="gsq_sum")
-            nc.tensor.matmul(gsq_sum[:], ones[:], folded["gsq"][:], start=True, stop=True)
             raw_inv_r = unit.tile([P, PIECE], F32, name="raw_inv_r")
-            nc.scalar.activation(raw_inv_r[:], xsq_sum[:], RSQRT, scale=1.0 / C)
-            inv_r = unit.tile([P, PIECE], F32, name="inv_r")
-            nc.vector.tensor_scalar_min(inv_r[:], raw_inv_r[:], C**0.5 / EPS)
+            for half in HALVES:
+                xsq_sum = psum_sum.tile([P, HALF], F32, name="xsq_sum", tag="sum")
+                nc.tensor.matmul(xsq_sum[:], ones[:], folded["xsq"][:, half], start=True, stop=True)
+                nc.scalar.activation(raw_inv_r[:, half], xsq_sum[:], RSQRT, scale=1.0 / C)
             u[piece] = unit.tile([P, CB, PIECE], BF16, name="u")
             for cb in range(CB):
-                nc.vector.scalar_tensor_tensor(
-                    u[piece][:, cb, :], x[piece][cb][:], gain[layer][:, cb : cb + 1], inv_r[:], MULT, MULT
-                )
-            inv_sq = unit.tile([P, PIECE], F32, name="inv_sq")
-            nc.scalar.activation(inv_sq[:], inv_r[:], SQUARE)
+                for half in HALVES:
+                    nc.vector.scalar_tensor_tensor(
+                        u[piece][:, cb, half], raw_inv_r[:, half], INV_R_CAP, gx[cb][:, half], MIN, MULT
+                    )
+            gsq_sum = psum_sum.tile([P, PIECE], F32, name="gsq_sum", tag="sum")
+            nc.tensor.matmul(gsq_sum[:], ones[:], folded["gsq"][:], start=True, stop=True)
+            gsq_over_r = unit.tile([P, PIECE], F32, name="gsq_over_r")
+            nc.vector.scalar_tensor_tensor(gsq_over_r[:], raw_inv_r[:], INV_R_CAP, gsq_sum[:], MIN, MULT)
             usq[piece] = unit.tile([P, PIECE], F32, name="usq")
-            nc.vector.tensor_tensor(usq[piece][:], gsq_sum[:], inv_sq[:], MULT)
+            nc.vector.scalar_tensor_tensor(usq[piece][:], raw_inv_r[:], INV_R_CAP, gsq_over_r[:], MIN, MULT)
 
         def project_in(layer, piece):
             a[piece] = unit.tile([P, FB, PIECE], BF16, name="a")
             if piece == 0:
-                wsq = psum_sum.tile([P, FB], F32, name="wsq")
+                wsq = psum_wsq.tile([P, FB], F32, name="wsq")
             for fb in range(FB):
                 h = psum_h.tile([P, PIECE], F32, name="h")
                 for cb in range(CB):

@@ -11,8 +11,10 @@ HALF = PIECE // 2
 HALVES = (slice(0, HALF), slice(HALF, PIECE))
 LAYERS = 2
 EPS = 1e-12
-INV_R_CAP = C**0.5 / EPS
+S_CAP = C**0.5 / EPS
 VECTOR_ROWS = LAYERS * (CB + FB)
+BANKS = 8
+EARLY = BANKS - len(HALVES)
 
 FLOPS = LAYERS * 2 * 2 * C * F * N
 
@@ -41,10 +43,7 @@ def tile_l2distancetransformer_b_kernel(
         tc.tile_pool(name="squares", bufs=CB) as squares,
         tc.tile_pool(name="win_squares", bufs=FB) as win_squares,
         tc.tile_pool(name="args", bufs=8) as args,
-        tc.psum_pool(name="psum_h", bufs=3) as psum_h,
-        tc.psum_pool(name="psum_acc", bufs=2) as psum_acc,
-        tc.psum_pool(name="psum_sum", bufs=2) as psum_sum,
-        tc.psum_pool(name="psum_wsq", bufs=1) as psum_wsq,
+        tc.psum_pool(name="psum", bufs=BANKS) as psum,
     ):
         offsets = held.tile([P, N // 16], U16, name="offsets")
         nc.sync.dma_start(offsets[:], offs)
@@ -58,7 +57,7 @@ def tile_l2distancetransformer_b_kernel(
             nc.scalar.dma_start(vector_rows[bin_row : bin_row + FB, :], bin_in[layer].rearrange("(b p) o -> b (p o)", p=P))
         identity = held.tile([2 * VECTOR_ROWS, 2 * VECTOR_ROWS], F32, name="identity")
         make_identity(nc, identity[:])
-        flipped = psum_wsq.tile([P, 2 * VECTOR_ROWS], F32, name="flipped", tag="wsq")
+        flipped = psum.tile([P, 2 * VECTOR_ROWS], F32, name="flipped", tag="bank")
         nc.tensor.transpose(flipped[:], vector_rows[:], identity[:])
         vectors = held.tile([P, 2 * VECTOR_ROWS], F32, name="vectors")
         nc.vector.tensor_copy(vectors[:], flipped[:])
@@ -73,25 +72,29 @@ def tile_l2distancetransformer_b_kernel(
         def load_pos(piece, cb):
             nc.sync.dma_start(pos_sb[piece][cb][:], pos[block(cb), piece * PIECE : (piece + 1) * PIECE])
 
-        def load_win(layer):
+        def load_win(layer, first_fb, end_fb):
+            columns = slice(first_fb * P, end_fb * P)
             for cb in range(CB):
-                nc.sync.dma_start(win_sb[layer][:, cb, :], win_in[layer][block(cb), :])
+                nc.sync.dma_start(win_sb[layer][:, cb, columns], win_in[layer][block(cb), columns])
 
         def load_wout(layer):
             nc.sync.dma_start(wout_sb[layer][:], wout_in[layer].rearrange("(b p) c -> p b c", p=P))
 
+        load_win(0, 0, EARLY)
         for cb in range(CB):
             nc.sync.dma_start(table[cb][:], emb[block(cb), :])
             load_pos(0, cb)
-        load_win(0)
+        load_win(0, EARLY, FB)
         for cb in range(CB):
             load_pos(1, cb)
         load_wout(0)
-        load_win(1)
+        load_win(1, 0, FB)
         load_wout(1)
 
         ones = held.tile([P, P], BF16, name="ones")
         nc.vector.memset(ones[:], 1.0)
+        minus_half = held.tile([P, P], BF16, name="minus_half")
+        nc.vector.memset(minus_half[:], -0.5)
         warm = held.tile([P, 1], F32, name="warm")
         nc.scalar.activation(warm[:], ones[:, 0:1], RSQRT)
         gain = [held.tile([P, CB], F32, name=f"gain{layer}") for layer in range(LAYERS)]
@@ -106,15 +109,23 @@ def tile_l2distancetransformer_b_kernel(
         gx = [None] * CB
         gsq_run = [None]
         folded = {}
+        raw_s = [None]
+        operand = [None] * CB
+        per_token = [None]
+        half_sq_terms = [None]
         win_sq = [None] * FB
-        u = [None] * PIECES
-        usq = [None] * PIECES
         a = [None] * PIECES
 
-        def square_win(layer):
-            for fb in range(FB):
+        def square_win(layer, first_fb, end_fb):
+            for fb in range(first_fb, end_fb):
                 win_sq[fb] = win_squares.tile([P, CB, P], BF16, name="win_sq")
                 nc.scalar.activation(win_sq[fb][:], win_sb[layer][:, :, block(fb)], SQUARE)
+
+        def bias_block(layer, fb):
+            wsq = psum.tile([P, 1], F32, name="wsq", tag="bank")
+            for cb in range(CB):
+                nc.tensor.matmul(wsq[:], win_sq[fb][:, cb, :], ones[:, 0:1], start=cb == 0, stop=cb == CB - 1)
+            nc.vector.tensor_tensor(bias[layer][:, fb : fb + 1], bin_sb[layer][:, fb : fb + 1], wsq[:], SUBTRACT)
 
         def embed_block(piece, cb):
             for half in HALVES:
@@ -124,14 +135,17 @@ def tile_l2distancetransformer_b_kernel(
                     x[piece][cb][:, half], table[cb][:].indirect(half_offsets), pos_sb[piece][cb][:, half], ADD
                 )
 
-        def square_block(layer, piece, cb):
+        def square_block(layer, piece, cb, first_unit):
             xsq[cb] = squares.tile([P, PIECE], F32, name="xsq")
             block_gain_sq = gain_sq[layer][:, cb : cb + 1]
             if cb == 0:
                 gsq_run[0] = unit.tile([P, PIECE], F32, name="gsq_run")
             if cb == CB - 1:
                 folded["xsq"] = unit.tile([P, PIECE], BF16, name="xsq_folded")
-                folded["gsq"] = unit.tile([P, PIECE], BF16, name="gsq_folded")
+                if first_unit:
+                    folded["gsq"] = unit.tile([P, PIECE], F32, name="gsq_folded_exact")
+                else:
+                    folded["gsq"] = unit.tile([P, PIECE], BF16, name="gsq_folded")
             for half in HALVES:
                 nc.scalar.activation(xsq[cb][:, half], x[piece][cb][:, half], SQUARE)
                 if cb == 0:
@@ -145,48 +159,66 @@ def tile_l2distancetransformer_b_kernel(
                     nc.vector.tensor_tensor(folded["xsq"][:, half], xsq[0][:, half], xsq[cb][:, half], ADD)
             if cb == CB - 1:
                 nc.vector.scalar_tensor_tensor(folded["gsq"][:], xsq[cb][:], block_gain_sq, gsq_run[0][:], MULT, ADD)
-            gx[cb] = squares.tile([P, PIECE], F32, name="gx")
-            nc.scalar.activation(gx[cb][:], x[piece][cb][:], COPY, scale=gain[layer][:, cb : cb + 1])
-
-        def finish_norm(layer, piece):
-            raw_inv_r = unit.tile([P, PIECE], F32, name="raw_inv_r")
+            if first_unit:
+                gx[cb] = squares.tile([P, PIECE], BF16, name="gx_rounded")
+            else:
+                gx[cb] = squares.tile([P, PIECE], F32, name="gx")
             for half in HALVES:
-                xsq_sum = psum_sum.tile([P, HALF], F32, name="xsq_sum", tag="sum")
-                nc.tensor.matmul(xsq_sum[:], ones[:], folded["xsq"][:, half], start=True, stop=True)
-                nc.scalar.activation(raw_inv_r[:, half], xsq_sum[:], RSQRT, scale=1.0 / C)
-            u[piece] = unit.tile([P, CB, PIECE], BF16, name="u")
-            for cb in range(CB):
-                for half in HALVES:
-                    nc.vector.scalar_tensor_tensor(
-                        u[piece][:, cb, half], raw_inv_r[:, half], INV_R_CAP, gx[cb][:, half], MIN, MULT
-                    )
-            gsq_sum = psum_sum.tile([P, PIECE], F32, name="gsq_sum", tag="sum")
-            nc.tensor.matmul(gsq_sum[:], ones[:], folded["gsq"][:], start=True, stop=True)
-            gsq_over_r = unit.tile([P, PIECE], F32, name="gsq_over_r")
-            nc.vector.scalar_tensor_tensor(gsq_over_r[:], raw_inv_r[:], INV_R_CAP, gsq_sum[:], MIN, MULT)
-            usq[piece] = unit.tile([P, PIECE], F32, name="usq")
-            nc.vector.scalar_tensor_tensor(usq[piece][:], raw_inv_r[:], INV_R_CAP, gsq_over_r[:], MIN, MULT)
+                nc.scalar.activation(gx[cb][:, half], x[piece][cb][:, half], COPY, scale=gain[layer][:, cb : cb + 1])
 
-        def project_in(layer, piece):
+        def reciprocal_root():
+            raw_s[0] = unit.tile([P, PIECE], F32, name="raw_s")
+            for half in HALVES:
+                xsq_sum = psum.tile([P, HALF], F32, name="xsq_sum", tag="bank")
+                nc.tensor.matmul(xsq_sum[:], ones[:], folded["xsq"][:, half], start=True, stop=True)
+                nc.scalar.activation(raw_s[0][:, half], xsq_sum[:], RSQRT, scale=1.0 / C)
+
+        def finish_first_norm():
+            reciprocal_root()
+            for cb in range(CB):
+                operand[cb] = gx[cb]
+            half_sq_terms[0] = unit.tile([P, PIECE], BF16, name="half_sq_terms")
+            nc.vector.scalar_tensor_tensor(half_sq_terms[0][:], raw_s[0][:], S_CAP, folded["gsq"][:], MIN, MULT)
+            per_token[0] = unit.tile([P, PIECE], F32, name="twice_s")
+            nc.vector.tensor_scalar(per_token[0][:], raw_s[0][:], S_CAP, 2.0, MIN, MULT)
+
+        def finish_norm():
+            reciprocal_root()
+            for cb in range(CB):
+                operand[cb] = squares.tile([P, PIECE], BF16, name="u")
+                for half in HALVES:
+                    nc.vector.scalar_tensor_tensor(operand[cb][:, half], raw_s[0][:, half], S_CAP, gx[cb][:, half], MIN, MULT)
+            gsq_sum = psum.tile([P, PIECE], F32, name="gsq_sum", tag="bank")
+            nc.tensor.matmul(gsq_sum[:], ones[:], folded["gsq"][:], start=True, stop=True)
+            s_q = unit.tile([P, PIECE], F32, name="s_q")
+            nc.vector.scalar_tensor_tensor(s_q[:], raw_s[0][:], S_CAP, gsq_sum[:], MIN, MULT)
+            per_token[0] = unit.tile([P, PIECE], F32, name="usq")
+            nc.vector.scalar_tensor_tensor(per_token[0][:], raw_s[0][:], S_CAP, s_q[:], MIN, MULT)
+
+        def project_in(layer, piece, begun):
+            first_unit = len(begun) > 0
             a[piece] = unit.tile([P, FB, PIECE], BF16, name="a")
-            if piece == 0:
-                wsq = psum_wsq.tile([P, FB], F32, name="wsq")
             for fb in range(FB):
-                h = psum_h.tile([P, PIECE], F32, name="h")
-                for cb in range(CB):
-                    nc.tensor.matmul(
-                        h[:], win_sb[layer][:, cb, block(fb)], u[piece][:, cb, :], start=cb == 0, stop=cb == CB - 1
-                    )
-                if piece == 0:
+                if fb < len(begun):
+                    h = begun[fb]
+                else:
+                    h = psum.tile([P, PIECE], F32, name="h", tag="bank")
                     for cb in range(CB):
                         nc.tensor.matmul(
-                            wsq[:, fb : fb + 1], win_sq[fb][:, cb, :], ones[:, 0:1], start=cb == 0, stop=cb == CB - 1
+                            h[:],
+                            win_sb[layer][:, cb, block(fb)],
+                            operand[cb][:],
+                            start=cb == 0,
+                            stop=cb == CB - 1 and not first_unit,
                         )
-                    nc.vector.tensor_tensor(
-                        bias[layer][:, fb : fb + 1], bin_sb[layer][:, fb : fb + 1], wsq[:, fb : fb + 1], SUBTRACT
-                    )
+                    if piece == 0:
+                        bias_block(layer, fb)
                 arg = args.tile([P, PIECE], F32, name="arg")
-                nc.vector.scalar_tensor_tensor(arg[:], h[:], 2.0, usq[piece][:], MULT, SUBTRACT)
+                if first_unit:
+                    nc.tensor.matmul(h[:], minus_half[:], half_sq_terms[0][:], start=False, stop=True)
+                    nc.vector.tensor_tensor(arg[:], h[:], per_token[0][:], MULT)
+                else:
+                    nc.vector.scalar_tensor_tensor(arg[:], h[:], 2.0, per_token[0][:], MULT, SUBTRACT)
                 nc.scalar.activation(a[piece][:, fb, :], arg[:], GELU, bias=bias[layer][:, fb : fb + 1])
                 if layer == 0 and piece + 1 < PIECES and fb % (FB // CB) == 0:
                     embed_block(piece + 1, fb // (FB // CB))
@@ -194,28 +226,37 @@ def tile_l2distancetransformer_b_kernel(
         def project_out(layer, piece, following):
             if following is not None:
                 for cb in range(CB):
-                    square_block(following[0], following[1], cb)
+                    square_block(following[0], following[1], cb, False)
             for cb in range(CB):
-                acc = psum_acc.tile([P, PIECE], F32, name="acc")
+                acc = psum.tile([P, PIECE], F32, name="acc", tag="bank")
                 for fb in range(FB):
                     nc.tensor.matmul(
                         acc[:], wout_sb[layer][:, fb, block(cb)], a[piece][:, fb, :], start=fb == 0, stop=fb == FB - 1
                     )
-                nc.vector.tensor_tensor(x[piece][cb][:], acc[:], x[piece][cb][:], ADD)
-                if layer == LAYERS - 1:
-                    nc.sync.dma_start(out[block(cb), piece * PIECE : (piece + 1) * PIECE], x[piece][cb][:])
+                for half in HALVES:
+                    nc.vector.tensor_tensor(x[piece][cb][:, half], acc[:, half], x[piece][cb][:, half], ADD)
+                    if layer == LAYERS - 1:
+                        first = piece * PIECE + half.start
+                        nc.sync.dma_start(out[block(cb), first : first + HALF], x[piece][cb][:, half])
                 if cb == 1 and following is not None:
-                    finish_norm(following[0], following[1])
+                    finish_norm()
 
-        units = [(layer, piece) for layer in range(LAYERS) for piece in range(PIECES)]
+        square_win(0, 0, EARLY)
+        for fb in range(EARLY):
+            bias_block(0, fb)
+        begun = [psum.tile([P, PIECE], F32, name=f"begun{fb}", tag="bank") for fb in range(EARLY)]
         for cb in range(CB):
             embed_block(0, cb)
-            square_block(0, 0, cb)
-        finish_norm(0, 0)
-        square_win(0)
+            square_block(0, 0, cb, True)
+            for fb in range(EARLY):
+                nc.tensor.matmul(begun[fb][:], win_sb[0][:, cb, block(fb)], gx[cb][:], start=cb == 0, stop=False)
+        finish_first_norm()
+        square_win(0, EARLY, FB)
+
+        units = [(layer, piece) for layer in range(LAYERS) for piece in range(PIECES)]
         for k, (layer, piece) in enumerate(units):
             following = units[k + 1] if k + 1 < len(units) else None
-            project_in(layer, piece)
+            project_in(layer, piece, begun if k == 0 else [])
             project_out(layer, piece, following)
             if piece == 0 and layer + 1 < LAYERS:
-                square_win(layer + 1)
+                square_win(layer + 1, 0, FB)

@@ -42,6 +42,7 @@ def tile_l2distancetransformer_b_kernel(
         tc.tile_pool(name="unit", bufs=1) as unit,
         tc.tile_pool(name="squares", bufs=CB) as squares,
         tc.tile_pool(name="win_squares", bufs=FB) as win_squares,
+        tc.tile_pool(name="win_folding", bufs=3) as win_folding,
         tc.tile_pool(name="args", bufs=8) as args,
         tc.psum_pool(name="psum", bufs=BANKS) as psum,
     ):
@@ -118,13 +119,23 @@ def tile_l2distancetransformer_b_kernel(
 
         def square_win(layer, first_fb, end_fb):
             for fb in range(first_fb, end_fb):
-                win_sq[fb] = win_squares.tile([P, CB, P], BF16, name="win_sq")
-                nc.scalar.activation(win_sq[fb][:], win_sb[layer][:, :, block(fb)], SQUARE)
+                if layer == 0:
+                    squared = win_squares.tile([P, CB, P], BF16, name="squared")
+                    nc.scalar.activation(squared[:], win_sb[layer][:, :, block(fb)], SQUARE)
+                    win_sq[fb] = [squared[:, cb, :] for cb in range(CB)]
+                else:
+                    exact = win_folding.tile([P, CB, P], F32, name="exact")
+                    nc.scalar.activation(exact[:], win_sb[layer][:, :, block(fb)], SQUARE)
+                    pairs = win_folding.tile([P, CB // 2, P], F32, name="pairs")
+                    nc.vector.tensor_tensor(pairs[:], exact[:, : CB // 2, :], exact[:, CB // 2 :, :], ADD)
+                    summed = win_squares.tile([P, P], BF16, name="summed")
+                    nc.vector.tensor_tensor(summed[:], pairs[:, 0, :], pairs[:, 1, :], ADD)
+                    win_sq[fb] = [summed[:]]
 
         def bias_block(layer, fb):
             wsq = psum.tile([P, 1], F32, name="wsq", tag="bank")
-            for cb in range(CB):
-                nc.tensor.matmul(wsq[:], win_sq[fb][:, cb, :], ones[:, 0:1], start=cb == 0, stop=cb == CB - 1)
+            for i, term in enumerate(win_sq[fb]):
+                nc.tensor.matmul(wsq[:], term, ones[:, 0:1], start=i == 0, stop=i == len(win_sq[fb]) - 1)
             nc.vector.tensor_tensor(bias[layer][:, fb : fb + 1], bin_sb[layer][:, fb : fb + 1], wsq[:], SUBTRACT)
 
         def embed_block(piece, cb):
@@ -159,12 +170,17 @@ def tile_l2distancetransformer_b_kernel(
                     nc.vector.tensor_tensor(folded["xsq"][:, half], xsq[0][:, half], xsq[cb][:, half], ADD)
             if cb == CB - 1:
                 nc.vector.scalar_tensor_tensor(folded["gsq"][:], xsq[cb][:], block_gain_sq, gsq_run[0][:], MULT, ADD)
+
+        def scale_block(layer, piece, cb, first_unit):
+            block_gain = gain[layer][:, cb : cb + 1]
             if first_unit:
                 gx[cb] = squares.tile([P, PIECE], BF16, name="gx_rounded")
+                for half in HALVES:
+                    nc.vector.tensor_scalar_mul(gx[cb][:, half], x[piece][cb][:, half], block_gain)
             else:
                 gx[cb] = squares.tile([P, PIECE], F32, name="gx")
-            for half in HALVES:
-                nc.scalar.activation(gx[cb][:, half], x[piece][cb][:, half], COPY, scale=gain[layer][:, cb : cb + 1])
+                for half in HALVES:
+                    nc.scalar.activation(gx[cb][:, half], x[piece][cb][:, half], COPY, scale=block_gain)
 
         def reciprocal_root():
             raw_s[0] = unit.tile([P, PIECE], F32, name="raw_s")
@@ -227,6 +243,7 @@ def tile_l2distancetransformer_b_kernel(
             if following is not None:
                 for cb in range(CB):
                     square_block(following[0], following[1], cb, False)
+                    scale_block(following[0], following[1], cb, False)
             for cb in range(CB):
                 acc = psum.tile([P, PIECE], F32, name="acc", tag="bank")
                 for fb in range(FB):
@@ -247,6 +264,7 @@ def tile_l2distancetransformer_b_kernel(
         begun = [psum.tile([P, PIECE], F32, name=f"begun{fb}", tag="bank") for fb in range(EARLY)]
         for cb in range(CB):
             embed_block(0, cb)
+            scale_block(0, 0, cb, True)
             square_block(0, 0, cb, True)
             for fb in range(EARLY):
                 nc.tensor.matmul(begun[fb][:], win_sb[0][:, cb, block(fb)], gx[cb][:], start=cb == 0, stop=False)

@@ -9,6 +9,7 @@ PIECE = 512
 PIECES = N // PIECE
 HALF = PIECE // 2
 HALVES = (slice(0, HALF), slice(HALF, PIECE))
+WHOLE = (slice(0, PIECE),)
 LAYERS = 2
 EPS = 1e-12
 S_CAP = C**0.5 / EPS
@@ -138,15 +139,15 @@ def tile_l2distancetransformer_b_kernel(
                 nc.tensor.matmul(wsq[:], term, ones[:, 0:1], start=i == 0, stop=i == len(win_sq[fb]) - 1)
             nc.vector.tensor_tensor(bias[layer][:, fb : fb + 1], bin_sb[layer][:, fb : fb + 1], wsq[:], SUBTRACT)
 
-        def embed_block(piece, cb):
-            for half in HALVES:
-                first = (piece * PIECE + half.start) // 16
-                half_offsets = offsets[:, first : first + HALF // 16]
+        def embed_block(piece, cb, parts):
+            for part in parts:
+                part_offsets = offsets[:, (piece * PIECE + part.start) // 16 : (piece * PIECE + part.stop) // 16]
                 nc.vector.tensor_tensor(
-                    x[piece][cb][:, half], table[cb][:].indirect(half_offsets), pos_sb[piece][cb][:, half], ADD
+                    x[piece][cb][:, part], table[cb][:].indirect(part_offsets), pos_sb[piece][cb][:, part], ADD
                 )
 
         def square_block(layer, piece, cb, first_unit):
+            parts = HALVES if first_unit else WHOLE
             xsq[cb] = squares.tile([P, PIECE], F32, name="xsq")
             block_gain_sq = gain_sq[layer][:, cb : cb + 1]
             if cb == 0:
@@ -157,17 +158,17 @@ def tile_l2distancetransformer_b_kernel(
                     folded["gsq"] = unit.tile([P, PIECE], F32, name="gsq_folded_exact")
                 else:
                     folded["gsq"] = unit.tile([P, PIECE], BF16, name="gsq_folded")
-            for half in HALVES:
-                nc.scalar.activation(xsq[cb][:, half], x[piece][cb][:, half], SQUARE)
+            for part in parts:
+                nc.scalar.activation(xsq[cb][:, part], x[piece][cb][:, part], SQUARE)
                 if cb == 0:
-                    nc.vector.tensor_scalar_mul(gsq_run[0][:, half], xsq[0][:, half], block_gain_sq)
+                    nc.vector.tensor_scalar_mul(gsq_run[0][:, part], xsq[0][:, part], block_gain_sq)
                 elif cb < CB - 1:
                     nc.vector.scalar_tensor_tensor(
-                        gsq_run[0][:, half], xsq[cb][:, half], block_gain_sq, gsq_run[0][:, half], MULT, ADD
+                        gsq_run[0][:, part], xsq[cb][:, part], block_gain_sq, gsq_run[0][:, part], MULT, ADD
                     )
-                    nc.vector.tensor_tensor(xsq[0][:, half], xsq[0][:, half], xsq[cb][:, half], ADD)
+                    nc.vector.tensor_tensor(xsq[0][:, part], xsq[0][:, part], xsq[cb][:, part], ADD)
                 else:
-                    nc.vector.tensor_tensor(folded["xsq"][:, half], xsq[0][:, half], xsq[cb][:, half], ADD)
+                    nc.vector.tensor_tensor(folded["xsq"][:, part], xsq[0][:, part], xsq[cb][:, part], ADD)
             if cb == CB - 1:
                 nc.vector.scalar_tensor_tensor(folded["gsq"][:], xsq[cb][:], block_gain_sq, gsq_run[0][:], MULT, ADD)
 
@@ -179,18 +180,17 @@ def tile_l2distancetransformer_b_kernel(
                     nc.vector.tensor_scalar_mul(gx[cb][:, half], x[piece][cb][:, half], block_gain)
             else:
                 gx[cb] = squares.tile([P, PIECE], F32, name="gx")
-                for half in HALVES:
-                    nc.scalar.activation(gx[cb][:, half], x[piece][cb][:, half], COPY, scale=block_gain)
+                nc.scalar.activation(gx[cb][:], x[piece][cb][:], COPY, scale=block_gain)
 
-        def reciprocal_root():
+        def reciprocal_root(parts):
             raw_s[0] = unit.tile([P, PIECE], F32, name="raw_s")
-            for half in HALVES:
-                xsq_sum = psum.tile([P, HALF], F32, name="xsq_sum", tag="bank")
-                nc.tensor.matmul(xsq_sum[:], ones[:], folded["xsq"][:, half], start=True, stop=True)
-                nc.scalar.activation(raw_s[0][:, half], xsq_sum[:], RSQRT, scale=1.0 / C)
+            for part in parts:
+                xsq_sum = psum.tile([P, part.stop - part.start], F32, name="xsq_sum", tag="bank")
+                nc.tensor.matmul(xsq_sum[:], ones[:], folded["xsq"][:, part], start=True, stop=True)
+                nc.scalar.activation(raw_s[0][:, part], xsq_sum[:], RSQRT, scale=1.0 / C)
 
         def finish_first_norm():
-            reciprocal_root()
+            reciprocal_root(HALVES)
             for cb in range(CB):
                 operand[cb] = gx[cb]
             half_sq_terms[0] = unit.tile([P, PIECE], BF16, name="half_sq_terms")
@@ -199,11 +199,10 @@ def tile_l2distancetransformer_b_kernel(
             nc.vector.tensor_scalar(per_token[0][:], raw_s[0][:], S_CAP, 2.0, MIN, MULT)
 
         def finish_norm():
-            reciprocal_root()
+            reciprocal_root(WHOLE)
             for cb in range(CB):
                 operand[cb] = squares.tile([P, PIECE], BF16, name="u")
-                for half in HALVES:
-                    nc.vector.scalar_tensor_tensor(operand[cb][:, half], raw_s[0][:, half], S_CAP, gx[cb][:, half], MIN, MULT)
+                nc.vector.scalar_tensor_tensor(operand[cb][:], raw_s[0][:], S_CAP, gx[cb][:], MIN, MULT)
             gsq_sum = psum.tile([P, PIECE], F32, name="gsq_sum", tag="bank")
             nc.tensor.matmul(gsq_sum[:], ones[:], folded["gsq"][:], start=True, stop=True)
             s_q = unit.tile([P, PIECE], F32, name="s_q")
@@ -237,7 +236,7 @@ def tile_l2distancetransformer_b_kernel(
                     nc.vector.scalar_tensor_tensor(arg[:], h[:], 2.0, per_token[0][:], MULT, SUBTRACT)
                 nc.scalar.activation(a[piece][:, fb, :], arg[:], GELU, bias=bias[layer][:, fb : fb + 1])
                 if layer == 0 and piece + 1 < PIECES and fb % (FB // CB) == 0:
-                    embed_block(piece + 1, fb // (FB // CB))
+                    embed_block(piece + 1, fb // (FB // CB), WHOLE)
 
         def project_out(layer, piece, following):
             if following is not None:
@@ -250,11 +249,11 @@ def tile_l2distancetransformer_b_kernel(
                     nc.tensor.matmul(
                         acc[:], wout_sb[layer][:, fb, block(cb)], a[piece][:, fb, :], start=fb == 0, stop=fb == FB - 1
                     )
-                for half in HALVES:
-                    nc.vector.tensor_tensor(x[piece][cb][:, half], acc[:, half], x[piece][cb][:, half], ADD)
+                for part in WHOLE if following is not None else HALVES:
+                    nc.vector.tensor_tensor(x[piece][cb][:, part], acc[:, part], x[piece][cb][:, part], ADD)
                     if layer == LAYERS - 1:
-                        first = piece * PIECE + half.start
-                        nc.sync.dma_start(out[block(cb), first : first + HALF], x[piece][cb][:, half])
+                        tokens = slice(piece * PIECE + part.start, piece * PIECE + part.stop)
+                        nc.sync.dma_start(out[block(cb), tokens], x[piece][cb][:, part])
                 if cb == 1 and following is not None:
                     finish_norm()
 
@@ -263,7 +262,7 @@ def tile_l2distancetransformer_b_kernel(
             bias_block(0, fb)
         begun = [psum.tile([P, PIECE], F32, name=f"begun{fb}", tag="bank") for fb in range(EARLY)]
         for cb in range(CB):
-            embed_block(0, cb)
+            embed_block(0, cb, HALVES)
             scale_block(0, 0, cb, True)
             square_block(0, 0, cb, True)
             for fb in range(EARLY):

@@ -243,19 +243,24 @@ def tile_l2distancetransformer_b_kernel(
                 for cb in range(CB):
                     square_block(following[0], following[1], cb, False)
                     scale_block(following[0], following[1], cb, False)
-            for cb in range(CB):
-                acc = psum.tile([P, PIECE], F32, name="acc", tag="bank")
-                for fb in range(FB):
-                    nc.tensor.matmul(
-                        acc[:], wout_sb[layer][:, fb, block(cb)], a[piece][:, fb, :], start=fb == 0, stop=fb == FB - 1
-                    )
-                for part in WHOLE if following is not None else HALVES:
-                    nc.vector.tensor_tensor(x[piece][cb][:, part], acc[:, part], x[piece][cb][:, part], ADD)
-                    if layer == LAYERS - 1:
-                        tokens = slice(piece * PIECE + part.start, piece * PIECE + part.stop)
-                        nc.sync.dma_start(out[block(cb), tokens], x[piece][cb][:, part])
-                if cb == 1 and following is not None:
+                steps = [(fb, cb) for fb in range(FB) for cb in range(CB)]
+            else:
+                steps = [(fb, cb) for cb in range(CB) for fb in range(FB)]
+            acc = [None] * CB
+            for i, (fb, cb) in enumerate(steps):
+                if i == len(steps) // 2 and following is not None:
                     finish_norm()
+                if fb == 0:
+                    acc[cb] = psum.tile([P, PIECE], F32, name="acc", tag="bank")
+                nc.tensor.matmul(
+                    acc[cb][:], wout_sb[layer][:, fb, block(cb)], a[piece][:, fb, :], start=fb == 0, stop=fb == FB - 1
+                )
+                if fb == FB - 1:
+                    for part in WHOLE if following is not None else HALVES:
+                        nc.vector.tensor_tensor(x[piece][cb][:, part], acc[cb][:, part], x[piece][cb][:, part], ADD)
+                        if layer == LAYERS - 1:
+                            tokens = slice(piece * PIECE + part.start, piece * PIECE + part.stop)
+                            nc.sync.dma_start(out[block(cb), tokens], x[piece][cb][:, part])
 
         square_win(0, 0, EARLY)
         for fb in range(EARLY):

@@ -15,7 +15,7 @@ EPS = 1e-12
 S_CAP = C**0.5 / EPS
 VECTOR_ROWS = LAYERS * (CB + FB)
 BANKS = 8
-EARLY = BANKS - len(HALVES)
+EARLY = BANKS - 1
 
 FLOPS = LAYERS * 2 * 2 * C * F * N
 
@@ -184,15 +184,13 @@ def tile_l2distancetransformer_b_kernel(
 
         def reciprocal_root(parts):
             raw_s[0] = unit.tile([P, PIECE], F32, name="raw_s")
+            xsq_sum = psum.tile([P, PIECE], F32, name="xsq_sum", tag="bank")
             for part in parts:
-                xsq_sum = psum.tile([P, part.stop - part.start], F32, name="xsq_sum", tag="bank")
-                nc.tensor.matmul(xsq_sum[:], ones[:], folded["xsq"][:, part], start=True, stop=True)
-                nc.scalar.activation(raw_s[0][:, part], xsq_sum[:], RSQRT, scale=1.0 / C)
+                nc.tensor.matmul(xsq_sum[:, part], ones[:], folded["xsq"][:, part], start=True, stop=True)
+                nc.scalar.activation(raw_s[0][:, part], xsq_sum[:, part], RSQRT, scale=1.0 / C)
 
         def finish_first_norm():
             reciprocal_root(HALVES)
-            for cb in range(CB):
-                operand[cb] = gx[cb]
             half_sq_terms[0] = unit.tile([P, PIECE], BF16, name="half_sq_terms")
             nc.vector.scalar_tensor_tensor(half_sq_terms[0][:], raw_s[0][:], S_CAP, folded["gsq"][:], MIN, MULT)
             per_token[0] = unit.tile([P, PIECE], F32, name="twice_s")
@@ -270,9 +268,11 @@ def tile_l2distancetransformer_b_kernel(
             embed_block(0, cb, HALVES)
             scale_block(0, 0, cb, True)
             square_block(0, 0, cb, True)
+            if cb == CB - 1:
+                finish_first_norm()
             for fb in range(EARLY):
                 nc.tensor.matmul(begun[fb][:], win_sb[0][:, cb, block(fb)], gx[cb][:], start=cb == 0, stop=False)
-        finish_first_norm()
+            operand[cb] = gx[cb]
         square_win(0, EARLY, FB)
 
         units = [(layer, piece) for layer in range(LAYERS) for piece in range(PIECES)]

@@ -208,7 +208,7 @@ def tile_l2distancetransformer_b_kernel(
             per_token[0] = unit.tile([P, PIECE], F32, name="usq")
             nc.vector.scalar_tensor_tensor(per_token[0][:], raw_s[0][:], S_CAP, s_q[:], MIN, MULT)
 
-        def project_in(layer, piece, begun):
+        def project_in(layer, piece, begun, following):
             first_unit = len(begun) > 0
             a[piece] = unit.tile([P, FB, PIECE], BF16, name="a")
             for fb in range(FB):
@@ -233,20 +233,21 @@ def tile_l2distancetransformer_b_kernel(
                 else:
                     nc.vector.scalar_tensor_tensor(arg[:], h[:], 2.0, per_token[0][:], MULT, SUBTRACT)
                 nc.scalar.activation(a[piece][:, fb, :], arg[:], GELU, bias=bias[layer][:, fb : fb + 1])
-                if layer == 0 and piece + 1 < PIECES and fb % (FB // CB) == 0:
-                    embed_block(piece + 1, fb // (FB // CB), WHOLE)
+                if following is not None and fb % (FB // CB) == 0:
+                    cb = fb // (FB // CB)
+                    if layer == 0 and piece + 1 < PIECES:
+                        embed_block(piece + 1, cb, WHOLE)
+                    square_block(following[0], following[1], cb, False)
+                    scale_block(following[0], following[1], cb, False)
 
         def project_out(layer, piece, following):
             if following is not None:
-                for cb in range(CB):
-                    square_block(following[0], following[1], cb, False)
-                    scale_block(following[0], following[1], cb, False)
                 steps = [(fb, cb) for fb in range(FB) for cb in range(CB)]
             else:
                 steps = [(fb, cb) for cb in range(CB) for fb in range(FB)]
             acc = [None] * CB
             for i, (fb, cb) in enumerate(steps):
-                if i == len(steps) // 2 and following is not None:
+                if i == len(steps) // 4 and following is not None:
                     finish_norm()
                 if fb == 0:
                     acc[cb] = psum.tile([P, PIECE], F32, name="acc", tag="bank")
@@ -278,7 +279,7 @@ def tile_l2distancetransformer_b_kernel(
         units = [(layer, piece) for layer in range(LAYERS) for piece in range(PIECES)]
         for k, (layer, piece) in enumerate(units):
             following = units[k + 1] if k + 1 < len(units) else None
-            project_in(layer, piece, begun if k == 0 else [])
+            project_in(layer, piece, begun if k == 0 else [], following)
             project_out(layer, piece, following)
             if piece == 0 and layer + 1 < LAYERS:
                 square_win(layer + 1, 0, FB)

@@ -10,6 +10,7 @@ PIECES = N // PIECE
 HALF = PIECE // 2
 HALVES = (slice(0, HALF), slice(HALF, PIECE))
 WHOLE = (slice(0, PIECE),)
+LAST_CUT = (slice(0, PIECE - PIECE // 4), slice(PIECE - PIECE // 4, PIECE))
 LAYERS = 2
 EPS = 1e-12
 S_CAP = C**0.5 / EPS
@@ -242,24 +243,26 @@ def tile_l2distancetransformer_b_kernel(
 
         def project_out(layer, piece, following):
             if following is not None:
-                steps = [(fb, cb) for fb in range(FB) for cb in range(CB)]
+                sums = [(cb, part) for cb in range(CB) for part in WHOLE]
+                steps = [(fb, cb, part) for fb in range(FB) for cb, part in sums]
             else:
-                steps = [(fb, cb) for cb in range(CB) for fb in range(FB)]
-            acc = [None] * CB
-            for i, (fb, cb) in enumerate(steps):
+                sums = [(cb, part) for cb in range(CB) for part in (LAST_CUT if cb == CB - 1 else WHOLE)]
+                steps = [(fb, cb, part) for cb, part in sums for fb in range(FB)]
+            acc = {}
+            for i, (fb, cb, part) in enumerate(steps):
                 if i == len(steps) // 4 and following is not None:
                     finish_norm()
                 if fb == 0:
-                    acc[cb] = psum.tile([P, PIECE], F32, name="acc", tag="bank")
+                    acc[cb, part.start] = psum.tile([P, part.stop - part.start], F32, name="acc", tag="bank")
+                total = acc[cb, part.start]
                 nc.tensor.matmul(
-                    acc[cb][:], wout_sb[layer][:, fb, block(cb)], a[piece][:, fb, :], start=fb == 0, stop=fb == FB - 1
+                    total[:], wout_sb[layer][:, fb, block(cb)], a[piece][:, fb, part], start=fb == 0, stop=fb == FB - 1
                 )
                 if fb == FB - 1:
-                    for part in WHOLE if following is not None else HALVES:
-                        nc.vector.tensor_tensor(x[piece][cb][:, part], acc[cb][:, part], x[piece][cb][:, part], ADD)
-                        if layer == LAYERS - 1:
-                            tokens = slice(piece * PIECE + part.start, piece * PIECE + part.stop)
-                            nc.sync.dma_start(out[block(cb), tokens], x[piece][cb][:, part])
+                    nc.vector.tensor_tensor(x[piece][cb][:, part], total[:], x[piece][cb][:, part], ADD)
+                    if layer == LAYERS - 1:
+                        tokens = slice(piece * PIECE + part.start, piece * PIECE + part.stop)
+                        nc.sync.dma_start(out[block(cb), tokens], x[piece][cb][:, part])
 
         square_win(0, 0, EARLY)
         for fb in range(EARLY):

@@ -96,8 +96,8 @@ def tile_l2distancetransformer_b_kernel(
 
         ones = held.tile([P, P], BF16, name="ones")
         nc.vector.memset(ones[:], 1.0)
-        minus_half = held.tile([P, P], BF16, name="minus_half")
-        nc.vector.memset(minus_half[:], -0.5)
+        minus_quarter = held.tile([P, P], BF16, name="minus_quarter")
+        nc.vector.memset(minus_quarter[:], -0.25)
         warm = held.tile([P, 1], F32, name="warm")
         nc.scalar.activation(warm[:], ones[:, 0:1], RSQRT)
         gain = [held.tile([P, CB], F32, name=f"gain{layer}") for layer in range(LAYERS)]
@@ -115,7 +115,7 @@ def tile_l2distancetransformer_b_kernel(
         raw_s = [None]
         operand = [None] * CB
         per_token = [None]
-        half_sq_terms = [None]
+        twice_sq_terms = [None]
         win_sq = [None] * FB
         a = [None] * PIECES
 
@@ -162,7 +162,7 @@ def tile_l2distancetransformer_b_kernel(
             for part in parts:
                 nc.scalar.activation(xsq[cb][:, part], x[piece][cb][:, part], SQUARE)
                 if cb == 0:
-                    nc.vector.tensor_scalar_mul(gsq_run[0][:, part], xsq[0][:, part], block_gain_sq)
+                    nc.scalar.activation(gsq_run[0][:, part], x[piece][cb][:, part], SQUARE, scale=gain[layer][:, 0:1])
                 elif cb < CB - 1:
                     nc.vector.scalar_tensor_tensor(
                         gsq_run[0][:, part], xsq[cb][:, part], block_gain_sq, gsq_run[0][:, part], MULT, ADD
@@ -183,31 +183,30 @@ def tile_l2distancetransformer_b_kernel(
                 gx[cb] = squares.tile([P, PIECE], F32, name="gx")
                 nc.scalar.activation(gx[cb][:], x[piece][cb][:], COPY, scale=block_gain)
 
-        def reciprocal_root(parts):
+        def reciprocal_root(parts, multiple):
             raw_s[0] = unit.tile([P, PIECE], F32, name="raw_s")
             xsq_sum = psum.tile([P, PIECE], F32, name="xsq_sum", tag="bank")
             for part in parts:
                 nc.tensor.matmul(xsq_sum[:, part], ones[:], folded["xsq"][:, part], start=True, stop=True)
-                nc.scalar.activation(raw_s[0][:, part], xsq_sum[:, part], RSQRT, scale=1.0 / C)
+                nc.scalar.activation(raw_s[0][:, part], xsq_sum[:, part], RSQRT, scale=1.0 / (C * multiple**2))
 
         def finish_first_norm():
-            reciprocal_root(HALVES)
-            half_sq_terms[0] = unit.tile([P, PIECE], BF16, name="half_sq_terms")
-            nc.vector.scalar_tensor_tensor(half_sq_terms[0][:], raw_s[0][:], S_CAP, folded["gsq"][:], MIN, MULT)
-            per_token[0] = unit.tile([P, PIECE], F32, name="twice_s")
-            nc.vector.tensor_scalar(per_token[0][:], raw_s[0][:], S_CAP, 2.0, MIN, MULT)
+            reciprocal_root(HALVES, 2.0)
+            twice_sq_terms[0] = unit.tile([P, PIECE], BF16, name="twice_sq_terms")
+            nc.vector.scalar_tensor_tensor(twice_sq_terms[0][:], raw_s[0][:], 2.0 * S_CAP, folded["gsq"][:], MIN, MULT)
+            per_token[0] = raw_s[0]
 
         def finish_norm():
-            reciprocal_root(WHOLE)
+            reciprocal_root(WHOLE, 1.0)
             for cb in range(CB):
                 operand[cb] = squares.tile([P, PIECE], BF16, name="u")
                 nc.vector.scalar_tensor_tensor(operand[cb][:], raw_s[0][:], S_CAP, gx[cb][:], MIN, MULT)
             gsq_sum = psum.tile([P, PIECE], F32, name="gsq_sum", tag="bank")
             nc.tensor.matmul(gsq_sum[:], ones[:], folded["gsq"][:], start=True, stop=True)
-            s_q = unit.tile([P, PIECE], F32, name="s_q")
-            nc.vector.scalar_tensor_tensor(s_q[:], raw_s[0][:], S_CAP, gsq_sum[:], MIN, MULT)
+            raw_s_sq = unit.tile([P, PIECE], F32, name="raw_s_sq")
+            nc.scalar.activation(raw_s_sq[:], raw_s[0][:], SQUARE)
             per_token[0] = unit.tile([P, PIECE], F32, name="usq")
-            nc.vector.scalar_tensor_tensor(per_token[0][:], raw_s[0][:], S_CAP, s_q[:], MIN, MULT)
+            nc.vector.scalar_tensor_tensor(per_token[0][:], raw_s_sq[:], S_CAP**2, gsq_sum[:], MIN, MULT)
 
         def project_in(layer, piece, begun, following):
             first_unit = len(begun) > 0
@@ -229,8 +228,8 @@ def tile_l2distancetransformer_b_kernel(
                         bias_block(layer, fb)
                 arg = args.tile([P, PIECE], F32, name="arg")
                 if first_unit:
-                    nc.tensor.matmul(h[:], minus_half[:], half_sq_terms[0][:], start=False, stop=True)
-                    nc.vector.tensor_tensor(arg[:], h[:], per_token[0][:], MULT)
+                    nc.tensor.matmul(h[:], minus_quarter[:], twice_sq_terms[0][:], start=False, stop=True)
+                    nc.vector.scalar_tensor_tensor(arg[:], per_token[0][:], 2.0 * S_CAP, h[:], MIN, MULT)
                 else:
                     nc.vector.scalar_tensor_tensor(arg[:], h[:], 2.0, per_token[0][:], MULT, SUBTRACT)
                 nc.scalar.activation(a[piece][:, fb, :], arg[:], GELU, bias=bias[layer][:, fb : fb + 1])

@@ -178,7 +178,10 @@ def tile_l2distancetransformer_b_kernel(
             if first_unit:
                 gx[cb] = squares.tile([P, PIECE], BF16, name="gx_rounded")
                 for half in HALVES:
-                    nc.vector.tensor_scalar_mul(gx[cb][:, half], x[piece][cb][:, half], block_gain)
+                    if cb < CB - 1:
+                        nc.scalar.activation(gx[cb][:, half], x[piece][cb][:, half], COPY, scale=block_gain)
+                    else:
+                        nc.vector.tensor_scalar_mul(gx[cb][:, half], x[piece][cb][:, half], block_gain)
             else:
                 gx[cb] = squares.tile([P, PIECE], F32, name="gx")
                 nc.scalar.activation(gx[cb][:], x[piece][cb][:], COPY, scale=block_gain)
@@ -269,8 +272,11 @@ def tile_l2distancetransformer_b_kernel(
         begun = [psum.tile([P, PIECE], F32, name=f"begun{fb}", tag="bank") for fb in range(EARLY)]
         for cb in range(CB):
             embed_block(0, cb, HALVES)
-            scale_block(0, 0, cb, True)
+            if cb == CB - 1:
+                scale_block(0, 0, cb, True)
             square_block(0, 0, cb, True)
+            if cb < CB - 1:
+                scale_block(0, 0, cb, True)
             if cb == CB - 1:
                 finish_first_norm()
             for fb in range(EARLY):

import concourse.mybir as mybir
from concourse.masks import make_identity

P = 128
C, S, N, F = 512, 2048, 1024, 1536
CB = C // P
FB = F // P
PIECE = 512
PIECES = N // PIECE
HALF = PIECE // 2
HALVES = (slice(0, HALF), slice(HALF, PIECE))
WHOLE = (slice(0, PIECE),)
LAST_CUT = (slice(0, PIECE - PIECE // 4), slice(PIECE - PIECE // 4, PIECE))
LAYERS = 2
EPS = 1e-12
S_CAP = C**0.5 / EPS
VECTOR_ROWS = LAYERS * (CB + FB)
BANKS = 8
EARLY = BANKS - 1

FLOPS = LAYERS * 2 * 2 * C * F * N

F32, BF16, U16 = mybir.dt.float32, mybir.dt.bfloat16, mybir.dt.uint16
ADD, SUBTRACT, MULT, MIN = mybir.AluOpType.add, mybir.AluOpType.subtract, mybir.AluOpType.mult, mybir.AluOpType.min
GELU = mybir.ActivationFunctionType.Gelu
SQUARE = mybir.ActivationFunctionType.Square
COPY = mybir.ActivationFunctionType.Copy
RSQRT = mybir.ActivationFunctionType.Abs_reciprocal_sqrt


def block(i):
    return slice(i * P, (i + 1) * P)


def tile_l2distancetransformer_b_kernel(
    tc, emb, pos, gam1, win1, bin1, wout1, gam2, win2, bin2, wout2, offs, out
):
    nc = tc.nc
    gam_in, win_in = (gam1, gam2), (win1, win2)
    bin_in, wout_in = (bin1, bin2), (wout1, wout2)

    with (
        tc.tile_pool(name="held", bufs=1) as held,
        tc.tile_pool(name="unit", bufs=1) as unit,
        tc.tile_pool(name="squares", bufs=CB) as squares,
        tc.tile_pool(name="win_squares", bufs=FB) as win_squares,
        tc.tile_pool(name="win_folding", bufs=3) as win_folding,
        tc.tile_pool(name="args", bufs=8) as args,
        tc.psum_pool(name="psum", bufs=BANKS) as psum,
    ):
        offsets = held.tile([P, N // 16], U16, name="offsets")
        nc.sync.dma_start(offsets[:], offs)

        vector_rows = held.tile([2 * VECTOR_ROWS, P], F32, name="vector_rows")
        nc.vector.memset(vector_rows[VECTOR_ROWS:, :], 0.0)
        for layer in range(LAYERS):
            gam_row = layer * (CB + FB)
            bin_row = gam_row + CB
            nc.scalar.dma_start(vector_rows[gam_row : gam_row + CB, :], gam_in[layer].rearrange("(b p) o -> b (p o)", p=P))
            nc.scalar.dma_start(vector_rows[bin_row : bin_row + FB, :], bin_in[layer].rearrange("(b p) o -> b (p o)", p=P))
        identity = held.tile([2 * VECTOR_ROWS, 2 * VECTOR_ROWS], F32, name="identity")
        make_identity(nc, identity[:])
        flipped = psum.tile([P, 2 * VECTOR_ROWS], F32, name="flipped", tag="bank")
        nc.tensor.transpose(flipped[:], vector_rows[:], identity[:])
        vectors = held.tile([P, 2 * VECTOR_ROWS], F32, name="vectors")
        nc.vector.tensor_copy(vectors[:], flipped[:])
        gam_sb = [vectors[:, layer * (CB + FB) : layer * (CB + FB) + CB] for layer in range(LAYERS)]
        bin_sb = [vectors[:, layer * (CB + FB) + CB : (layer + 1) * (CB + FB)] for layer in range(LAYERS)]

        table = [held.tile([P, S], F32, name=f"table{cb}") for cb in range(CB)]
        pos_sb = [[held.tile([P, PIECE], F32, name=f"pos{piece}_{cb}") for cb in range(CB)] for piece in range(PIECES)]
        win_sb = [held.tile([P, CB, F], BF16, name=f"win{layer}") for layer in range(LAYERS)]
        wout_sb = [held.tile([P, FB, C], BF16, name=f"wout{layer}") for layer in range(LAYERS)]

        def load_pos(piece, cb):
            nc.sync.dma_start(pos_sb[piece][cb][:], pos[block(cb), piece * PIECE : (piece + 1) * PIECE])

        def load_win(layer, first_fb, end_fb):
            columns = slice(first_fb * P, end_fb * P)
            for cb in range(CB):
                nc.sync.dma_start(win_sb[layer][:, cb, columns], win_in[layer][block(cb), columns])

        def load_wout(layer):
            nc.sync.dma_start(wout_sb[layer][:], wout_in[layer].rearrange("(b p) c -> p b c", p=P))

        load_win(0, 0, EARLY)
        for cb in range(CB):
            nc.sync.dma_start(table[cb][:], emb[block(cb), :])
            load_pos(0, cb)
        load_win(0, EARLY, FB)
        for cb in range(CB):
            load_pos(1, cb)
        load_wout(0)
        load_win(1, 0, FB)
        load_wout(1)

        ones = held.tile([P, P], BF16, name="ones")
        nc.vector.memset(ones[:], 1.0)
        minus_quarter = held.tile([P, P], BF16, name="minus_quarter")
        nc.vector.memset(minus_quarter[:], -0.25)
        warm = held.tile([P, 1], F32, name="warm")
        nc.scalar.activation(warm[:], ones[:, 0:1], RSQRT)
        gain = [held.tile([P, CB], F32, name=f"gain{layer}") for layer in range(LAYERS)]
        gain_sq = [held.tile([P, CB], F32, name=f"gain_sq{layer}") for layer in range(LAYERS)]
        for layer in range(LAYERS):
            nc.vector.tensor_scalar_add(gain[layer][:], gam_sb[layer][:], 1.0)
            nc.vector.tensor_tensor(gain_sq[layer][:], gain[layer][:], gain[layer][:], MULT)
        bias = [held.tile([P, FB], F32, name=f"bias{layer}") for layer in range(LAYERS)]

        x = [[held.tile([P, PIECE], F32, name=f"x{piece}_{cb}") for cb in range(CB)] for piece in range(PIECES)]
        xsq = [None] * CB
        gx = [None] * CB
        gsq_run = [None]
        folded = {}
        raw_s = [None]
        operand = [None] * CB
        per_token = [None]
        twice_sq_terms = [None]
        win_sq = [None] * FB
        a = [None] * PIECES

        def square_win(layer, first_fb, end_fb):
            for fb in range(first_fb, end_fb):
                if layer == 0:
                    squared = win_squares.tile([P, CB, P], BF16, name="squared")
                    nc.scalar.activation(squared[:], win_sb[layer][:, :, block(fb)], SQUARE)
                    win_sq[fb] = [squared[:, cb, :] for cb in range(CB)]
                else:
                    exact = win_folding.tile([P, CB, P], F32, name="exact")
                    nc.scalar.activation(exact[:], win_sb[layer][:, :, block(fb)], SQUARE)
                    pairs = win_folding.tile([P, CB // 2, P], F32, name="pairs")
                    nc.vector.tensor_tensor(pairs[:], exact[:, : CB // 2, :], exact[:, CB // 2 :, :], ADD)
                    summed = win_squares.tile([P, P], BF16, name="summed")
                    nc.vector.tensor_tensor(summed[:], pairs[:, 0, :], pairs[:, 1, :], ADD)
                    win_sq[fb] = [summed[:]]

        def bias_block(layer, fb):
            wsq = psum.tile([P, 1], F32, name="wsq", tag="bank")
            for i, term in enumerate(win_sq[fb]):
                nc.tensor.matmul(wsq[:], term, ones[:, 0:1], start=i == 0, stop=i == len(win_sq[fb]) - 1)
            nc.vector.tensor_tensor(bias[layer][:, fb : fb + 1], bin_sb[layer][:, fb : fb + 1], wsq[:], SUBTRACT)

        def embed_block(piece, cb, parts):
            for part in parts:
                part_offsets = offsets[:, (piece * PIECE + part.start) // 16 : (piece * PIECE + part.stop) // 16]
                nc.vector.tensor_tensor(
                    x[piece][cb][:, part], table[cb][:].indirect(part_offsets), pos_sb[piece][cb][:, part], ADD
                )

        def square_block(layer, piece, cb, first_unit):
            parts = HALVES if first_unit else WHOLE
            xsq[cb] = squares.tile([P, PIECE], F32, name="xsq")
            block_gain_sq = gain_sq[layer][:, cb : cb + 1]
            if cb == 0:
                gsq_run[0] = unit.tile([P, PIECE], F32, name="gsq_run")
            if cb == CB - 1:
                folded["xsq"] = unit.tile([P, PIECE], BF16, name="xsq_folded")
                if first_unit:
                    folded["gsq"] = unit.tile([P, PIECE], F32, name="gsq_folded_exact")
                else:
                    folded["gsq"] = unit.tile([P, PIECE], BF16, name="gsq_folded")
            for part in parts:
                nc.scalar.activation(xsq[cb][:, part], x[piece][cb][:, part], SQUARE)
                if cb == 0:
                    nc.scalar.activation(gsq_run[0][:, part], x[piece][cb][:, part], SQUARE, scale=gain[layer][:, 0:1])
                elif cb < CB - 1:
                    nc.vector.scalar_tensor_tensor(
                        gsq_run[0][:, part], xsq[cb][:, part], block_gain_sq, gsq_run[0][:, part], MULT, ADD
                    )
                    nc.vector.tensor_tensor(xsq[0][:, part], xsq[0][:, part], xsq[cb][:, part], ADD)
                else:
                    nc.vector.tensor_tensor(folded["xsq"][:, part], xsq[0][:, part], xsq[cb][:, part], ADD)
            if cb == CB - 1:
                nc.vector.scalar_tensor_tensor(folded["gsq"][:], xsq[cb][:], block_gain_sq, gsq_run[0][:], MULT, ADD)

        def scale_block(layer, piece, cb, first_unit):
            block_gain = gain[layer][:, cb : cb + 1]
            if first_unit:
                gx[cb] = squares.tile([P, PIECE], BF16, name="gx_rounded")
                for half in HALVES:
                    if cb < CB - 1:
                        nc.scalar.activation(gx[cb][:, half], x[piece][cb][:, half], COPY, scale=block_gain)
                    else:
                        nc.vector.tensor_scalar_mul(gx[cb][:, half], x[piece][cb][:, half], block_gain)
            else:
                gx[cb] = squares.tile([P, PIECE], F32, name="gx")
                nc.scalar.activation(gx[cb][:], x[piece][cb][:], COPY, scale=block_gain)

        def reciprocal_root(parts, multiple):
            raw_s[0] = unit.tile([P, PIECE], F32, name="raw_s")
            xsq_sum = psum.tile([P, PIECE], F32, name="xsq_sum", tag="bank")
            for part in parts:
                nc.tensor.matmul(xsq_sum[:, part], ones[:], folded["xsq"][:, part], start=True, stop=True)
                nc.scalar.activation(raw_s[0][:, part], xsq_sum[:, part], RSQRT, scale=1.0 / (C * multiple**2))

        def finish_first_norm():
            reciprocal_root(HALVES, 2.0)
            twice_sq_terms[0] = unit.tile([P, PIECE], BF16, name="twice_sq_terms")
            nc.vector.scalar_tensor_tensor(twice_sq_terms[0][:], raw_s[0][:], 2.0 * S_CAP, folded["gsq"][:], MIN, MULT)
            per_token[0] = raw_s[0]

        def finish_norm():
            reciprocal_root(WHOLE, 1.0)
            for cb in range(CB):
                operand[cb] = squares.tile([P, PIECE], BF16, name="u")
                nc.vector.scalar_tensor_tensor(operand[cb][:], raw_s[0][:], S_CAP, gx[cb][:], MIN, MULT)
            gsq_sum = psum.tile([P, PIECE], F32, name="gsq_sum", tag="bank")
            nc.tensor.matmul(gsq_sum[:], ones[:], folded["gsq"][:], start=True, stop=True)
            raw_s_sq = unit.tile([P, PIECE], F32, name="raw_s_sq")
            nc.scalar.activation(raw_s_sq[:], raw_s[0][:], SQUARE)
            per_token[0] = unit.tile([P, PIECE], F32, name="usq")
            nc.vector.scalar_tensor_tensor(per_token[0][:], raw_s_sq[:], S_CAP**2, gsq_sum[:], MIN, MULT)

        def project_in(layer, piece, begun, following):
            first_unit = len(begun) > 0
            a[piece] = unit.tile([P, FB, PIECE], BF16, name="a")
            for fb in range(FB):
                if fb < len(begun):
                    h = begun[fb]
                else:
                    h = psum.tile([P, PIECE], F32, name="h", tag="bank")
                    for cb in range(CB):
                        nc.tensor.matmul(
                            h[:],
                            win_sb[layer][:, cb, block(fb)],
                            operand[cb][:],
                            start=cb == 0,
                            stop=cb == CB - 1 and not first_unit,
                        )
                    if piece == 0:
                        bias_block(layer, fb)
                arg = args.tile([P, PIECE], F32, name="arg")
                if first_unit:
                    nc.tensor.matmul(h[:], minus_quarter[:], twice_sq_terms[0][:], start=False, stop=True)
                    nc.vector.scalar_tensor_tensor(arg[:], per_token[0][:], 2.0 * S_CAP, h[:], MIN, MULT)
                else:
                    nc.vector.scalar_tensor_tensor(arg[:], h[:], 2.0, per_token[0][:], MULT, SUBTRACT)
                nc.scalar.activation(a[piece][:, fb, :], arg[:], GELU, bias=bias[layer][:, fb : fb + 1])
                if following is not None and fb % (FB // CB) == 0:
                    cb = fb // (FB // CB)
                    if layer == 0 and piece + 1 < PIECES:
                        embed_block(piece + 1, cb, WHOLE)
                    square_block(following[0], following[1], cb, False)
                    scale_block(following[0], following[1], cb, False)

        def project_out(layer, piece, following):
            if following is not None:
                sums = [(cb, part) for cb in range(CB) for part in WHOLE]
                steps = [(fb, cb, part) for fb in range(FB) for cb, part in sums]
            else:
                sums = [(cb, part) for cb in range(CB) for part in (LAST_CUT if cb == CB - 1 else WHOLE)]
                steps = [(fb, cb, part) for cb, part in sums for fb in range(FB)]
            acc = {}
            for i, (fb, cb, part) in enumerate(steps):
                if i == len(steps) // 4 and following is not None:
                    finish_norm()
                if fb == 0:
                    acc[cb, part.start] = psum.tile([P, part.stop - part.start], F32, name="acc", tag="bank")
                total = acc[cb, part.start]
                nc.tensor.matmul(
                    total[:], wout_sb[layer][:, fb, block(cb)], a[piece][:, fb, part], start=fb == 0, stop=fb == FB - 1
                )
                if fb == FB - 1:
                    nc.vector.tensor_tensor(x[piece][cb][:, part], total[:], x[piece][cb][:, part], ADD)
                    if layer == LAYERS - 1:
                        tokens = slice(piece * PIECE + part.start, piece * PIECE + part.stop)
                        nc.sync.dma_start(out[block(cb), tokens], x[piece][cb][:, part])

        square_win(0, 0, EARLY)
        for fb in range(EARLY):
            bias_block(0, fb)
        begun = [psum.tile([P, PIECE], F32, name=f"begun{fb}", tag="bank") for fb in range(EARLY)]
        for cb in range(CB):
            embed_block(0, cb, HALVES)
            if cb == CB - 1:
                scale_block(0, 0, cb, True)
            square_block(0, 0, cb, True)
            if cb < CB - 1:
                scale_block(0, 0, cb, True)
            if cb == CB - 1:
                finish_first_norm()
            for fb in range(EARLY):
                nc.tensor.matmul(begun[fb][:], win_sb[0][:, cb, block(fb)], gx[cb][:], start=cb == 0, stop=False)
            operand[cb] = gx[cb]
        square_win(0, EARLY, FB)

        units = [(layer, piece) for layer in range(LAYERS) for piece in range(PIECES)]
        for k, (layer, piece) in enumerate(units):
            following = units[k + 1] if k + 1 < len(units) else None
            project_in(layer, piece, begun if k == 0 else [], following)
            project_out(layer, piece, following)
            if piece == 0 and layer + 1 < LAYERS:
                square_win(layer + 1, 0, FB)
